import numpy as np
import ml_dtypes


def mxq(x, axis, fmt="e4m3"):
    dtype, down = {"e4m3": (ml_dtypes.float8_e4m3fn, 7), "e5m2": (ml_dtypes.float8_e5m2, 14)}[fmt]
    v = np.moveaxis(np.asarray(x, np.float32).astype(ml_dtypes.bfloat16).astype(np.float64), axis, -1)
    blocks = v.reshape(v.shape[:-1] + (-1, 32))
    amax = np.abs(blocks).max(-1, keepdims=True)
    byte = np.maximum(np.where(amax > 0, np.frexp(amax)[1] - 1 + 127, 0) - down, 1)
    scale = np.exp2(byte - 127.0)
    codes = (blocks / scale).astype(np.float32).astype(dtype).astype(np.float64)
    return np.moveaxis((codes * scale).reshape(v.shape), -1, axis)


WIDE = False


def mx_kscale(k):
    if not WIDE:
        return np.ones(k)
    levels = np.array([18, -18])
    if k % 512:
        return np.exp2(np.random.permutation(np.resize(levels, k // 32))).repeat(32)
    a = np.empty((k // 512, 16))
    for p in range(k // 512):
        a[p, :8] = np.random.permutation(np.resize(levels, 8))
        for g in range(8):
            far = levels[np.abs(levels - a[p, g]) >= 10]
            a[p, g + 8] = far[np.random.randint(len(far))]
    return np.exp2(a.ravel()).repeat(32)


BF16 = ml_dtypes.bfloat16


def bf(x):
    return np.asarray(x, np.float32).astype(BF16)


def f64(x):
    return np.asarray(x).astype(np.float64)


L, B, S, E, H, D = 2, 4, 256, 1024, 4, 128
T = B * S
J = H * D
THETA = 1000000.0
EPS = 1e-6


def rotate_half(x):
    x1, x2 = x[..., : D // 2], x[..., D // 2 :]
    return np.concatenate([-x2, x1], axis=-1)


def rope_cos_sin(n):
    inv_freq = 1.0 / (THETA ** (np.arange(0, D, 2) / D))
    freqs = np.arange(n)[:, None] * inv_freq[None, :]
    emb = np.concatenate([freqs, freqs], axis=-1)
    return np.cos(emb), np.sin(emb)


def setup_inputs():
    s = mx_kscale(T)
    u = mx_kscale(2 * J)
    uk = np.repeat(u[0] ** np.array([1.0, -1.0] * (H // 2)), D)
    uv = u[J:]
    x0 = bf(np.random.standard_normal((B, S, E)))
    ls = bf(np.sqrt(EPS) * np.exp2(np.random.uniform(-1.0, 1.0, L)))
    ln_w = bf(1.0 + 0.1 * np.random.standard_normal((L, E)))
    wk0 = bf(np.random.standard_normal((L, J, E)) / np.sqrt(E))
    wv0 = bf(np.random.standard_normal((L, J, E)) / np.sqrt(E))
    kn_w = bf(1.0 + 0.1 * np.random.standard_normal((L, D)))
    g = np.random.standard_normal((2, L, B, H, S, D)) * np.exp2(np.random.randint(-6, 1, (B, 1, S, 1)))
    g = g / s.reshape(B, 1, S, 1) * np.stack([uk, uv]).reshape(2, 1, 1, H, 1, D)
    scaled = f64(x0)[None] * f64(ls)[:, None, None, None]
    inv_rms = 1.0 / np.sqrt(np.mean(scaled * scaled, axis=-1) + EPS)
    normed = scaled * inv_rms[..., None] * f64(ln_w)[:, None, None, :]
    k = normed @ f64(wk0).transpose(0, 2, 1)[:, None]
    return {"image_context": bf(f64(x0) * s.reshape(B, S, 1)),
            "layer_scales": ls,
            "ln_w": ln_w,
            "Wk": bf(f64(wk0) / uk[:, None]),
            "Wv": bf(f64(wv0) / uv[:, None]),
            "kn_w": kn_w,
            "k": np.asarray(k, np.float32),
            "inv_rms": np.asarray(inv_rms, np.float32),
            "grad_out": bf(g)}


def reference(image_context, layer_scales, ln_w, Wk, Wv, kn_w, k, inv_rms, grad_out):
    x = f64(image_context).reshape(T, E)
    ls = f64(layer_scales)[:, None, None]
    lw = f64(ln_w)[:, None, :]
    r = f64(inv_rms).reshape(L, T, 1)
    g = f64(grad_out)
    cos, sin = rope_cos_sin(S)
    gk = g[0] * cos - rotate_half(g[0] * sin)
    h = gk.transpose(0, 1, 3, 2, 4) * f64(kn_w)[:, None, None, None, :]
    kf = f64(k).reshape(L, B, S, H, D)
    rk = 1.0 / np.sqrt(np.mean(kf * kf, axis=-1, keepdims=True) + EPS)
    khat = kf * rk
    dk = (rk * (h - khat * np.mean(h * khat, axis=-1, keepdims=True))).reshape(L, T, J)
    dv = g[1].transpose(0, 1, 3, 2, 4).reshape(L, T, J)
    dkv = np.concatenate([dk, dv], axis=2)
    wkv = np.concatenate([f64(Wk), f64(Wv)], axis=1)
    dnormed = mxq(dkv, 2, "e5m2") @ mxq(wkv, 1, "e4m3")
    xhat = x[None] * ls * r
    normed = xhat * lw
    dwk = mxq(dk, 1, "e5m2").transpose(0, 2, 1) @ mxq(normed, 1, "e4m3")
    dh = dnormed * lw
    dscaled = r * (dh - xhat * np.mean(dh * xhat, axis=-1, keepdims=True))
    dx = np.sum(dscaled * ls, axis=0).reshape(B, S, E)
    return dx, dwk

@@ -1,0 +1,703 @@
+import math
+from contextlib import ExitStack
+
+import concourse.mybir as mybir
+from concourse.masks import make_identity
+
+L, B, S, E, H, D = 2, 4, 256, 1024, 4, 128
+T = B * S
+J = H * D
+THETA = 1000000.0
+EPS = 1e-6
+FLOPS = 2 * L * T * (2 * J) * E + 2 * L * J * T * E
+
+F32 = mybir.dt.float32
+BF16 = mybir.dt.bfloat16
+I32 = mybir.dt.int32
+U32 = mybir.dt.uint32
+U8 = mybir.dt.uint8
+E4 = mybir.dt.float8_e4m3fn_x4
+E5 = mybir.dt.float8_e5m2_x4
+ALU = mybir.AluOpType
+ACT = mybir.ActivationFunctionType
+AX = mybir.AxisListType
+
+P = 128
+G = 2
+NC = E // P
+HALF = D // 2
+NHI = 24
+NPE = 8
+GRID = 2.0**18
+
+
+def tile_qwenextension_v2_v_kernel(
+    tc, image_context, layer_scales, ln_w, Wk, Wv, kn_w, k, inv_rms, grad_out, out_0, out_1
+):
+    nc = tc.nc
+    x_hbm = image_context.rearrange("b s e -> (b s) e").rearrange("(g p j) e -> g p j e", g=G, j=4)
+    o0_hbm = out_0.rearrange("b s e -> (b s) e").rearrange("(g p j) e -> g j p e", g=G, j=4)
+    k_hbm = k.rearrange("l b s f -> l (b s) f").rearrange("l (g p j) f -> l g p (j f)", g=G, j=4)
+    w_hbm = [Wk, Wv]
+
+    with ExitStack() as ctx:
+        ctx.enter_context(tc.manual_schedule())
+        keep = ctx.enter_context(tc.tile_pool(name="keep", bufs=1))
+        work = ctx.enter_context(tc.tile_pool(name="work", bufs=2))
+        psum = ctx.enter_context(tc.psum_pool(name="psum", bufs=6))
+        with tc.tile_pool(name="early", bufs=1) as early:
+
+            n_codes = [[keep.tile([P, E], U32, name="nc%d%d" % (l, g), align_bytes=64) for g in range(G)] for l in range(L)]
+            n_scales = [[keep.tile([P, E], U8, name="ns%d%d" % (l, g), align_bytes=64) for g in range(G)] for l in range(L)]
+            w_codes = [[keep.tile([P, E], U32, name="wc%d%d" % (l, m), align_bytes=64) for m in range(2)] for l in range(L)]
+            w_scales = [[keep.tile([P, E], U8, name="ws%d%d" % (l, m), align_bytes=64) for m in range(2)] for l in range(L)]
+            t_codes = [[keep.tile([P, J], U32, name="tc%d%d" % (l, g), align_bytes=64) for g in range(G)] for l in range(L)]
+            t_scales = [[keep.tile([P, J], U8, name="ts%d%d" % (l, g), align_bytes=64) for g in range(G)] for l in range(L)]
+            f_codes = {}
+            f_scales = {}
+            for l in range(L):
+                for g in range(G):
+                    for m in range(2):
+                        f_codes[l, g, m] = keep.tile([P, 512], U32, name="fc%d%d%d" % (l, g, m), align_bytes=64)
+                        f_scales[l, g, m] = keep.tile([P, 512], U8, name="fs%d%d%d" % (l, g, m), align_bytes=64)
+
+            st = {}
+            units = [(0, 0), (1, 0), (0, 1), (1, 1)]
+
+            def load_k(u):
+                l, g = units[u]
+                kt = work.tile([P, 4, J], F32, name="kt", tag="kt", bufs=3)
+                nc.sync.dma_start(out=kt[:].rearrange("p j f -> p (j f)"), in_=k_hbm[l, g])
+                st["k", u] = kt
+
+            def load_g(u):
+                l, g = units[u]
+                gt = work.tile([P, H, 4, D], BF16, name="gt", tag="gt")
+                for bb in range(2):
+                    nc.sync.dma_start(
+                        out=gt[64 * bb : 64 * (bb + 1)].rearrange("q h j d -> q h (j d)"),
+                        in_=grad_out[0, l, 2 * g + bb].rearrange("h (q j) d -> q h (j d)", j=4),
+                    )
+                st["g", u] = gt
+
+            def load_dv(u):
+                l, g = units[u]
+                dv = work.tile([P, 4, J], BF16, name="dv", tag="dv")
+                for i in range(4):
+                    src = grad_out[1, l, 2 * g + i // 2, :, P * (i % 2) : P * (i % 2 + 1), :]
+                    nc.sync.dma_start(out=dv[:, i, :].rearrange("q (h d) -> q h d", h=H), in_=src.rearrange("h q d -> q h d"))
+                st["dv", u] = dv
+
+            def load_w(w):
+                l, m = divmod(w, 2)
+                raw = early.tile([P, 4, E], BF16, name="wraw", tag="wraw", bufs=2)
+                nc.sync.dma_start(
+                    out=raw[:].rearrange("p j e -> p (j e)"), in_=w_hbm[m][l].rearrange("(p j) e -> p (j e)", j=4)
+                )
+                st["w", w] = raw
+
+            def interleave(dst, src):
+                nc.scalar.copy(dst.rearrange("p (c i) t -> p c t i", i=4), src.rearrange("p t (c i) -> p c t i", i=4))
+
+            def w_group(i):
+                w, hh = divmod(i, 2)
+                grouped = early.tile([P, 512, 4], BF16, name="wint", tag="wint", bufs=2, align_bytes=64)
+                interleave(grouped[:], st["w", w][:, :, 512 * hh : 512 * (hh + 1)])
+                st["wint", i] = grouped
+
+            def w_quant(i):
+                w, hh = divmod(i, 2)
+                l, m = divmod(w, 2)
+                cols = slice(512 * hh, 512 * (hh + 1))
+                nc.vector.quantize_mx(
+                    w_codes[l][m][:, cols].bitcast(E4), w_scales[l][m][:, cols], st["wint", i][:].rearrange("p e t -> p (e t)")
+                )
+
+            def x_turn(c):
+                xt = psum.tile([P, 2, 2, G, P], BF16, name="xt", tag="bank")
+                for g in range(G):
+                    for j in range(4):
+                        nc.tensor.transpose(xt[:, j % 2, j // 2, g, :], x[g][:, j, P * c : P * (c + 1)], ident_b[:])
+                st["xt", c] = xt
+
+            def normed_mul(c, l):
+                nt = early.tile([P, 512, 2], BF16, name="nt", tag="nt", bufs=4)
+                nc.vector.scalar_tensor_tensor(
+                    nt[:],
+                    st["xt", c][:].rearrange("q e u g p -> q (u g p) e"),
+                    lwls[:, l, c : c + 1],
+                    r_row[l][:].rearrange("q u g p e -> q (u g p) e"),
+                    ALU.mult,
+                    ALU.mult,
+                )
+                st["nt", c, l] = nt
+
+            def normed_turn(c, l):
+                words = st["nt", c, l][:].rearrange("q w e -> q (w e)").bitcast(F32)
+                bank = psum.tile([P, G, 2, P], F32, name="nb", tag="bank")
+                for g in range(G):
+                    for u in range(2):
+                        w0 = 256 * u + P * g
+                        nc.tensor.transpose(bank[:, g, u, :], words[:, w0 : w0 + P], ident_f[:])
+                if c % 2 == 0:
+                    st["nint", c // 2, l] = early.tile([P, G, 1024], BF16, name="nint", tag="nint", bufs=4, align_bytes=64)
+                nint = st["nint", c // 2, l]
+                dst = nint[:].bitcast(F32).rearrange("p g (cc e u) -> p g cc e u", cc=2, u=2)[:, :, c % 2]
+                nc.scalar.copy(dst, bank[:].rearrange("p g u e -> p g e u"))
+
+            def normed_quant(cp, l):
+                cols = slice(2 * P * cp, 2 * P * (cp + 1))
+                for g in range(G):
+                    nc.vector.quantize_mx(
+                        n_codes[l][g][:, cols].bitcast(E4), n_scales[l][g][:, cols], st["nint", cp, l][:, g, :]
+                    )
+
+            def square_sums(u, j):
+                kt = st["k", u]
+                if j == 0:
+                    st["ss", u] = work.tile([P, 16], F32, name="ss", tag="ss")
+                ss = st["ss", u]
+                for h in range(H):
+                    junk = work.tile([P, D], F32, name="sqj", tag="sqj")
+                    nc.scalar.activation(
+                        junk[:], kt[:, j, D * h : D * (h + 1)], ACT.Square, accum_out=ss[:, 4 * j + h : 4 * j + h + 1]
+                    )
+
+            def stats(u, part):
+                if part == 0:
+                    for nm in ("var", "rec", "y0", "tmp", "rk", "kap"):
+                        st[nm, u] = work.tile([P, 16], F32, name=nm, tag=nm)
+                var, rec, y0, tmp, rk, kap = [st[nm, u] for nm in ("var", "rec", "y0", "tmp", "rk", "kap")]
+                if part == 0:
+                    nc.vector.tensor_scalar(var[:], st["ss", u][:], 1.0 / D, EPS, ALU.mult, ALU.add)
+                elif part == 1:
+                    nc.vector.reciprocal(rec[:], var[:])
+                    nc.scalar.activation(y0[:], rec[:], ACT.Sqrt)
+                elif part == 2:
+                    nc.vector.tensor_tensor(tmp[:], y0[:], y0[:], ALU.mult)
+                    nc.vector.tensor_scalar(kap[:], rec[:], -1.0 / D, None, ALU.mult)
+                elif part == 3:
+                    nc.vector.scalar_tensor_tensor(tmp[:], tmp[:], -0.5, var[:], ALU.mult, ALU.mult)
+                else:
+                    nc.vector.scalar_tensor_tensor(rk[:], tmp[:], 1.5, y0[:], ALU.add, ALU.mult)
+
+            def rope_products(n):
+                u, j = divmod(n, 4)
+                l = units[u][0]
+                t = work.tile([P, H, 2, D], F32, name="t", tag="t", bufs=3)
+                for h in range(H):
+                    nc.vector.scalar_tensor_tensor(
+                        t[:, h],
+                        st["g", u][:, h, j].unsqueeze(1).to_broadcast([P, 2, D]),
+                        st["rk", u][:, 4 * j + h : 4 * j + h + 1],
+                        rope[l][:, j],
+                        ALU.mult,
+                        ALU.mult,
+                    )
+                st["t", n] = t
+
+            def rope_sum(n):
+                t = st["t", n]
+                if n >= NPE:
+                    return
+                hb = psum.tile([P, H, D], F32, name="hb", tag="hb", bufs=2)
+                nc.tensor.matmul(hb[:], lhsT=ident_f[:], rhs=t[:, :, 0, :], start=True, stop=False)
+                nc.tensor.matmul(hb[:, :, 0:HALF], lhsT=ident_f[:], rhs=t[:, :, 1, HALF:D], start=False, stop=False)
+                nc.tensor.matmul(hb[:, :, HALF:D], lhsT=ident_f[:], rhs=t[:, :, 1, 0:HALF], start=False, stop=True)
+                st["hb", n] = hb
+
+            def rope_add(n):
+                t = st["t", n]
+                if n < NPE:
+                    return
+                for a in range(2):
+                    here = t[:, :, 0, HALF * a : HALF * (a + 1)]
+                    nc.vector.tensor_tensor(here, here, t[:, :, 1, HALF * (1 - a) : HALF * (2 - a)], ALU.add)
+                st["hb", n] = t[:, :, 0, :]
+
+            def key_grad(n):
+                u, j = divmod(n, 4)
+                if j == 0:
+                    st["dk", u] = work.tile([P, 4, J], BF16, name="dk", tag="dk")
+                    st["coef", u] = work.tile([P, 16], F32, name="coef", tag="coef")
+                kt, kap, dk, coef, t, hb = st["k", u], st["kap", u], st["dk", u], st["coef", u], st["t", n], st["hb", n]
+                for h in range(H):
+                    s = slice(4 * j + h, 4 * j + h + 1)
+                    kh = kt[:, j, D * h : D * (h + 1)]
+                    nc.vector.scalar_tensor_tensor(
+                        t[:, h, 1], hb[:, h], kap[:, s], kh, ALU.mult, ALU.mult, accum_out=coef[:, s]
+                    )
+                for h in range(H):
+                    s = slice(4 * j + h, 4 * j + h + 1)
+                    kh = kt[:, j, D * h : D * (h + 1)]
+                    nc.vector.scalar_tensor_tensor(dk[:, j, D * h : D * (h + 1)], kh, coef[:, s], hb[:, h], ALU.mult, ALU.add)
+
+            def dk_turn(u, jp):
+                if jp == 0:
+                    st["dt", u, 0] = work.tile([P, 4, P, 4], BF16, name="dt", tag="dt", align_bytes=64)
+                dtw = st["dt", u, 0][:].rearrange("p j r t -> p (j r t)").bitcast(F32).rearrange("p (j r u) -> p j r u", j=4, u=2)
+                bank = psum.tile([P, 2, 2, P], F32, name="kb", tag="bank")
+                for jj in range(2):
+                    words = st["dk", u][:, 2 * jp + jj, :].bitcast(F32)
+                    for v in range(2):
+                        nc.tensor.transpose(bank[:, jj, v, :], words[:, v : 256 : 2], ident_f[:])
+                nc.scalar.copy(dtw[:, 2 * jp : 2 * jp + 2], bank[:].rearrange("p j u r -> p j r u"))
+
+            def dv_turn(u, ip):
+                if ip == 0:
+                    st["dt", u, 1] = work.tile([P, 4, P, 4], BF16, name="dt", tag="dt", align_bytes=64)
+                dtw = st["dt", u, 1][:].rearrange("p j r t -> p (j r t)").bitcast(F32)
+                dtw = dtw.rearrange("p (j ip ii q u) -> p j ip ii q u", j=4, ip=2, ii=2, u=2)
+                bank = psum.tile([P, 2, 2, P], F32, name="vb", tag="bank")
+                for ii in range(2):
+                    words = st["dv", u][:, 2 * ip + ii, :].bitcast(F32)
+                    for v in range(2):
+                        nc.tensor.transpose(bank[:, ii, v, :], words[:, v : 256 : 2], ident_f[:])
+                nc.scalar.copy(dtw[:, :, ip], bank[:].rearrange("p ii u (q j) -> p j ii q u", j=4))
+
+            def feature_quant(u, m):
+                l, g = units[u]
+                nc.vector.quantize_mx(
+                    f_codes[l, g, m][:].bitcast(E5), f_scales[l, g, m][:], st["dt", u, m][:].rearrange("p j r t -> p (j r t)")
+                )
+
+            def dk_group(u):
+                grouped = work.tile([P, J, 4], BF16, name="dki", tag="dki", bufs=1, align_bytes=64)
+                interleave(grouped[:], st["dk", u][:])
+                st["dki", u] = grouped
+
+            def token_quant(u):
+                l, g = units[u]
+                nc.vector.quantize_mx(
+                    t_codes[l][g][:].bitcast(E5), t_scales[l][g][:], st["dki", u][:].rearrange("p f t -> p (f t)")
+                )
+
+            def dnormed(g, c, l):
+                cols = slice(P * c, P * (c + 1))
+                bank = psum.tile([P, 512], F32, name="dn", tag="bank")
+                for m in range(2):
+                    nc.tensor.matmul_mx(
+                        bank[:],
+                        lhsT=w_codes[l][m][:, cols].bitcast(E4),
+                        lhsT_scale=w_scales[l][m][:, cols],
+                        rhs=f_codes[l, g, m][:].bitcast(E5),
+                        rhs_scale=f_scales[l, g, m][:],
+                        start=(m == 0),
+                        stop=(m == 1),
+                    )
+                st["dn", c, l] = bank
+
+            def dnormed_out(g, c, l):
+                at = st["late"].tile([P, 512], F32, name="at", tag="at", bufs=16)
+                bank = st["dn", c, l]
+                if l == 0:
+                    nc.vector.scalar_tensor_tensor(at[:], bank[:], lwls[:, 0, c : c + 1], rho_row[:, g, :], ALU.mult, ALU.mult)
+                else:
+                    nc.scalar.activation(at[:], bank[:], ACT.Copy, scale=lwls[:, 1, c : c + 1])
+                st["at", l, c] = at
+
+            def back_turn(g, j, hh):
+                late = st["late"]
+                toks = slice(P * j, P * (j + 1))
+                if hh == 0:
+                    st["part", j] = late.tile([P, 3], F32, name="part", tag="part", bufs=4)
+                    st["negc", j] = late.tile([P, 1], F32, name="negc", tag="negc", bufs=4)
+                    st["o1", j] = late.tile([P, E], F32, name="o1", tag="o1", bufs=4)
+                both = psum.tile([P, 4, P], F32, name="both", tag="bank")
+                for cc in range(4):
+                    for l in range(L):
+                        nc.tensor.matmul(
+                            both[:, cc, :],
+                            lhsT=st["at", l, 4 * hh + cc][:, toks],
+                            rhs=ident_f[:],
+                            start=(l == 0),
+                            stop=(l == 1),
+                            is_transpose=True,
+                        )
+                nc.scalar.activation(
+                    st["o1", j][:, 512 * hh : 512 * (hh + 1)],
+                    both[:].rearrange("p c e -> p (c e)"),
+                    ACT.Copy,
+                    scale=rcol[:, 1, g, j : j + 1],
+                )
+                one = psum.tile([P, 4, P], F32, name="one", tag="bank")
+                for cc in range(4):
+                    nc.tensor.transpose(one[:, cc, :], st["at", 1, 4 * hh + cc][:, toks], ident_f[:])
+                st["one", j, hh] = one
+
+            def dot_one(g, j, hh):
+                junk = st["late"].tile([P, 512], F32, name="junk", tag="junk", bufs=2)
+                nc.vector.scalar_tensor_tensor(
+                    junk[:],
+                    st["one", j, hh][:].rearrange("p c e -> p (c e)"),
+                    beta[:, 4 * g + j : 4 * g + j + 1],
+                    x[g][:, j, 512 * hh : 512 * (hh + 1)],
+                    ALU.mult,
+                    ALU.mult,
+                    accum_out=st["part", j][:, hh : hh + 1],
+                )
+
+            def dot_both(g, j):
+                junk = st["late"].tile([P, E], F32, name="junk", tag="junk", bufs=2)
+                nc.vector.scalar_tensor_tensor(
+                    junk[:],
+                    st["o1", j][:],
+                    alpha[:, 4 * g + j : 4 * g + j + 1],
+                    x[g][:, j, :],
+                    ALU.mult,
+                    ALU.mult,
+                    accum_out=st["part", j][:, 2:3],
+                )
+
+            def dot_sum(j):
+                nc.vector.tensor_reduce(st["negc", j][:], st["part", j][:], AX.X, ALU.add)
+
+            def finish(g, j):
+                o1 = st["o1", j]
+                nc.vector.scalar_tensor_tensor(o1[:], x[g][:, j, :], st["negc", j][:], o1[:], ALU.mult, ALU.add)
+                nc.sync.dma_start(out=o0_hbm[g, j], in_=o1[:])
+
+            def weight_grad(l, ft):
+                rows = slice(P * ft, P * (ft + 1))
+                stage = st["late"].tile([P, E], F32, name="dws", tag="dws", bufs=2)
+                for hh in range(2):
+                    cols = slice(512 * hh, 512 * (hh + 1))
+                    bank = psum.tile([P, 512], F32, name="dw", tag="bank")
+                    for g in range(G):
+                        nc.tensor.matmul_mx(
+                            bank[:],
+                            lhsT=t_codes[l][g][:, rows].bitcast(E5),
+                            lhsT_scale=t_scales[l][g][:, rows],
+                            rhs=n_codes[l][g][:, cols].bitcast(E4),
+                            rhs_scale=n_scales[l][g][:, cols],
+                            start=(g == 0),
+                            stop=(g == G - 1),
+                        )
+                    nc.scalar.copy(stage[:, cols], bank[:])
+                nc.sync.dma_start(out=out_1[l, rows, :], in_=stage[:])
+
+            pos = early.tile([P, 4], F32, name="pos")
+            nc.gpsimd.iota(pos[:], pattern=[[1, 4]], base=0, channel_multiplier=4, allow_small_or_imprecise_dtypes=True)
+            lwrows = early.tile([P, P], BF16, name="lwrows")
+            nc.gpsimd.memset(lwrows[:], 0.0)
+            ident_f = keep.tile([P, P], F32, name="ident_f")
+            make_identity(nc, ident_f[:])
+            ident_b = keep.tile([P, P], BF16, name="ident_b")
+            make_identity(nc, ident_b[:])
+
+            rcol = keep.tile([P, L, G, 4], F32, name="rcol")
+            nc.scalar.dma_start(
+                out=rcol[:].rearrange("p l g j -> p (l g) j"),
+                in_=inv_rms.rearrange("l b s -> (l b s)").rearrange("(m p j) -> p m j", p=P, j=4),
+            )
+            ls = keep.tile([P, L], BF16, name="ls")
+            nc.scalar.dma_start(out=ls[:], in_=layer_scales.partition_broadcast(P))
+            nc.scalar.dma_start(out=lwrows[0 : L * NC, :], in_=ln_w.rearrange("l (c p) -> (l c) p", p=P))
+            x = [keep.tile([P, 4, E], BF16, name="x%d" % g) for g in range(G)]
+
+            def load_x(hh):
+                for g in range(G):
+                    cols = slice(512 * hh, 512 * (hh + 1))
+                    nc.sync.dma_start(out=x[g][:, :, cols], in_=x_hbm[g][:, :, cols])
+
+            load_x(0)
+            load_k(0)
+            kw = early.tile([P, L, D], BF16, name="kw")
+            nc.sync.dma_start(
+                out=kw[:].rearrange("p l d -> p (l d)"), in_=kn_w.rearrange("l d -> (l d)").partition_broadcast(P)
+            )
+            load_w(0)
+            load_g(0)
+            load_x(1)
+            load_w(1)
+            load_k(1)
+            load_dv(0)
+            load_g(1)
+            load_dv(1)
+
+            onezero = early.tile([P, 2], F32, name="onezero")
+            nc.vector.memset(onezero[:, 0:1], 1.0)
+            nc.vector.memset(onezero[:, 1:2], 0.0)
+            wrap = early.tile([P, 4], F32, name="wrap")
+            freq = early.tile([P, 2, HALF], F32, name="freq")
+            turns = [THETA ** (-i / HALF) / (2 * math.pi) for i in range(HALF)]
+            for i in range(NHI):
+                hi = int(turns[i] * GRID) / GRID
+                nc.vector.tensor_scalar(freq[:, :, i], onezero[:], hi, turns[i] - hi, ALU.min, ALU.max)
+            nc.vector.tensor_scalar(wrap[:], pos[:], float(S), -float(S), ALU.is_ge, ALU.mult)
+            for i in range(NHI, HALF, 2):
+                nc.vector.tensor_scalar(freq[:, 1, i : i + 2], onezero[:], turns[i], turns[i + 1], ALU.min, ALU.max)
+                if i == NHI:
+                    nc.vector.tensor_tensor(pos[:], pos[:], wrap[:], ALU.add)
+            whole = early.tile([P, 4, NHI], F32, name="whole")
+            whole_i = early.tile([P, 4, NHI], I32, name="whole_i")
+            phase = early.tile([P, 2, 4, HALF], F32, name="phase")
+            nphase = early.tile([P, 2, 4, HALF], F32, name="nphase")
+            rflat = rcol[:].rearrange("p l g j -> p l (g j)")
+            rsq = early.tile([P, L, 8], F32, name="rsq")
+            rho = early.tile([P, 8], F32, name="rho")
+            alpha = keep.tile([P, 8], F32, name="alpha")
+            beta = keep.tile([P, 8], F32, name="beta")
+            lwls = keep.tile([P, L, NC], F32, name="lwls")
+            lw_ps = psum.tile([P, P], BF16, name="lw_ps", tag="bank")
+            r_row = [early.tile([P, 2, G, P, 2], F32, name="r_row%d" % l) for l in range(L)]
+            for l in range(L):
+                for u in range(2):
+                    bank = psum.tile([P, G, 2, P], F32, name="rb", tag="bank")
+                    for g in range(G):
+                        for e2 in range(2):
+                            col = rcol[:, l, g, 2 * u + e2 : 2 * u + e2 + 1]
+                            nc.tensor.transpose(bank[:, g, e2, :], col.to_broadcast([P, P]), ident_f[:])
+                    nc.scalar.copy(r_row[l][:, u], bank[:].rearrange("q g e p -> q g p e"))
+            nc.tensor.transpose(lw_ps[:], lwrows[:], ident_b[:])
+            nc.vector.tensor_tensor(
+                whole[:],
+                pos[:].unsqueeze(2).to_broadcast([P, 4, NHI]),
+                freq[:, 0, 0:NHI].unsqueeze(1).to_broadcast([P, 4, NHI]),
+                ALU.mult,
+            )
+            nc.vector.tensor_tensor(
+                phase[:, 0],
+                pos[:].unsqueeze(2).to_broadcast([P, 4, HALF]),
+                freq[:, 1, :].unsqueeze(1).to_broadcast([P, 4, HALF]),
+                ALU.mult,
+            )
+            nc.vector.tensor_copy(whole_i[:], whole[:])
+            nc.vector.reciprocal(rho[:], rflat[:, 1, :])
+            nc.vector.tensor_tensor(whole[:], whole[:], whole_i[:], ALU.subtract)
+            nc.vector.tensor_tensor(rsq[:], rflat, ls[:].unsqueeze(2).to_broadcast([P, L, 8]), ALU.mult)
+            nc.vector.tensor_tensor(phase[:, 0, :, 0:NHI], phase[:, 0, :, 0:NHI], whole[:], ALU.add)
+            nc.vector.tensor_tensor(rho[:], rho[:], rflat[:, 0, :], ALU.mult)
+            nc.vector.tensor_scalar(phase[:, 1], phase[:, 0], 0.25, None, ALU.add)
+            nc.vector.tensor_tensor(rsq[:], rsq[:], rsq[:], ALU.mult)
+            flat = "p a j i -> p (a j i)"
+            nc.vector.scalar_tensor_tensor(
+                nphase[:].rearrange(flat), phase[:].rearrange(flat), 0.5, phase[:].rearrange(flat), ALU.is_ge, ALU.subtract
+            )
+            for l in range(L):
+                nc.vector.tensor_scalar(lwls[:, l, :], lw_ps[:, l * NC : (l + 1) * NC], ls[:, l : l + 1], None, ALU.mult)
+            nc.vector.tensor_tensor(beta[:], rsq[:, 0, :], rsq[:, 1, :], ALU.subtract)
+            nc.vector.tensor_scalar(alpha[:], rsq[:, 0, :], -1.0 / E, None, ALU.mult)
+            nc.vector.scalar_tensor_tensor(beta[:], beta[:], 1.0 / E, rflat[:, 1, :], ALU.mult, ALU.mult)
+            cos_t = early.tile([P, 4, HALF], F32, name="cos_t")
+            sin_t = early.tile([P, 4, 2, HALF], F32, name="sin_t")
+            nc.scalar.activation(cos_t[:], nphase[:, 1], ACT.Sin, scale=-2 * math.pi)
+            nc.scalar.activation(sin_t[:, :, 0, :], nphase[:, 0], ACT.Sin, scale=2 * math.pi)
+            nc.scalar.activation(sin_t[:, :, 1, :], nphase[:, 0], ACT.Sin, scale=-2 * math.pi)
+            rope = [keep.tile([P, 4, 2, D], F32, name="rope%d" % l) for l in range(L)]
+            for l in range(L):
+                nc.gpsimd.tensor_tensor(
+                    rope[l][:, :, 0, :].rearrange("p j (a i) -> p j a i", a=2),
+                    cos_t[:].unsqueeze(2).to_broadcast([P, 4, 2, HALF]),
+                    kw[:, l, :].rearrange("p (a i) -> p a i", a=2).unsqueeze(1).to_broadcast([P, 4, 2, HALF]),
+                    ALU.mult,
+                )
+                for a in range(2):
+                    nc.gpsimd.tensor_tensor(
+                        rope[l][:, :, 1, HALF * a : HALF * (a + 1)],
+                        sin_t[:, :, a, :],
+                        kw[:, l, HALF * (1 - a) : HALF * (2 - a)].unsqueeze(1).to_broadcast([P, 4, HALF]),
+                        ALU.mult,
+                    )
+            rho_row = keep.tile([P, G, 4 * P], F32, name="rho_row")
+
+            def spread_rho(g):
+                bank = psum.tile([P, 4, P], F32, name="rhob", tag="bank")
+                for j in range(4):
+                    col = rho[:, 4 * g + j : 4 * g + j + 1]
+                    nc.tensor.transpose(bank[:, j, :], col.to_broadcast([P, P]), ident_f[:])
+                nc.scalar.copy(rho_row[:, g, :], bank[:].rearrange("q j p -> q (j p)"))
+
+            x_turn(0)
+            x_turn(1)
+            for j in range(4):
+                square_sums(0, j)
+            normed_mul(0, 0)
+            normed_mul(0, 1)
+            x_turn(2)
+            normed_mul(1, 0)
+            normed_mul(1, 1)
+            stats(0, 0)
+            normed_turn(0, 0)
+            normed_mul(2, 0)
+            stats(0, 1)
+            normed_turn(0, 1)
+            normed_mul(2, 1)
+            x_turn(3)
+            normed_turn(1, 0)
+            normed_turn(1, 1)
+            stats(0, 2)
+            w_group(0)
+            normed_quant(0, 0)
+            stats(0, 3)
+            normed_quant(0, 1)
+            stats(0, 4)
+            for n in range(9):
+                u, j = divmod(n, 4)
+                c = n + 3
+                rope_products(n)
+                if n < 6:
+                    normed_turn(c - 1, 0)
+                    normed_turn(c - 1, 1)
+                rope_sum(n)
+                if c + 1 < NC:
+                    x_turn(c + 1)
+                if n < 4:
+                    square_sums(1, n)
+                elif n < 8:
+                    square_sums(2, n - 4)
+                if n < 7:
+                    w_group(n + 1)
+                if n > 0:
+                    key_grad(n - 1)
+                if n in (2, 4, 6):
+                    load_w(n // 2 + 1) if n < 6 else None
+                if n == 2:
+                    load_k(2)
+                if n == 4:
+                    load_g(2)
+                    load_k(3)
+                rope_add(n)
+                if n < 8:
+                    w_quant(n)
+                if j == 3:
+                    stats(u + 1, 0)
+                if c < NC:
+                    normed_mul(c, 0)
+                if j == 3:
+                    stats(u + 1, 1)
+                if c < NC:
+                    normed_mul(c, 1)
+                if j == 3:
+                    stats(u + 1, 2)
+                if n in (1, 3, 5):
+                    normed_quant((n + 1) // 2, 0)
+                if j == 3:
+                    stats(u + 1, 3)
+                if n in (1, 3, 5):
+                    normed_quant((n + 1) // 2, 1)
+                if j == 3:
+                    stats(u + 1, 4)
+                if n in (1, 2):
+                    dv_turn(0, n - 1)
+                if n == 3:
+                    feature_quant(0, 1)
+                if n in (2, 4):
+                    dk_turn(0, n // 2 - 1)
+                if n == 5:
+                    feature_quant(0, 0)
+                    dk_group(0)
+                    load_dv(2)
+                if n in (5, 6):
+                    dv_turn(1, n - 5)
+                if n == 7:
+                    feature_quant(1, 1)
+                    token_quant(0)
+                    spread_rho(0)
+                    spread_rho(1)
+                if n in (6, 8):
+                    dk_turn(1, n // 2 - 3)
+                if n == 8:
+                    load_g(3)
+                    load_dv(3)
+        st["late"] = ctx.enter_context(tc.tile_pool(name="late", bufs=1))
+        for n in range(9, 17):
+            if n < 16:
+                rope_products(n)
+            if n == 9:
+                feature_quant(1, 0)
+                dk_group(1)
+            if n == 9:
+                for jj in range(4):
+                    square_sums(3, jj)
+            if n < 13:
+                for c in (2 * (n - 9), 2 * (n - 9) + 1):
+                    dnormed(0, c, 0)
+                    dnormed(0, c, 1)
+                    dnormed_out(0, c, 1)
+            else:
+                back_turn(0, n - 13, 0)
+                back_turn(0, n - 13, 1)
+            if n < 16:
+                rope_sum(n)
+            if n == 11:
+                stats(3, 0)
+            key_grad(n - 1)
+            if n == 11:
+                stats(3, 1)
+            if n < 16:
+                rope_add(n)
+            if n == 11:
+                stats(3, 2)
+            if n < 13:
+                dnormed_out(0, 2 * (n - 9), 0)
+                if n == 11:
+                    stats(3, 3)
+                dnormed_out(0, 2 * (n - 9) + 1, 0)
+                if n == 11:
+                    stats(3, 4)
+            else:
+                dot_one(0, n - 13, 0)
+                dot_one(0, n - 13, 1)
+            if n == 10:
+                token_quant(1)
+            if n in (9, 10):
+                dv_turn(2, n - 9)
+            if n == 11:
+                feature_quant(2, 1)
+            if n in (10, 12):
+                dk_turn(2, n // 2 - 5)
+            if n == 13:
+                feature_quant(2, 0)
+                dk_group(2)
+            if n in (13, 14):
+                dv_turn(3, n - 13)
+            if n == 14:
+                token_quant(2)
+            if n == 15:
+                feature_quant(3, 1)
+            if n in (14, 16):
+                dk_turn(3, n // 2 - 7)
+            if n == 16:
+                dk_group(3)
+            if n >= 15:
+                weight_grad(0, 2 * (n - 15))
+                weight_grad(0, 2 * (n - 15) + 1)
+        dot_both(0, 0)
+        dot_both(0, 1)
+        dot_sum(0)
+        feature_quant(3, 0)
+        finish(0, 0)
+        for c in range(NC):
+            dnormed(1, c, 0)
+            dnormed(1, c, 1)
+            dnormed_out(1, c, 1)
+            if c == 0:
+                dot_sum(1)
+                token_quant(3)
+            if c == 1:
+                finish(0, 1)
+            if c in (2, 4):
+                dot_both(0, c // 2 + 1)
+            if c in (4, 6):
+                finish(0, c // 2)
+            dnormed_out(1, c, 0)
+            if c in (2, 4):
+                dot_sum(c // 2 + 1)
+        for jj in range(5):
+            if jj < 4:
+                back_turn(1, jj, 0)
+                back_turn(1, jj, 1)
+            if jj > 0:
+                dot_both(1, jj - 1)
+            if jj < 4:
+                dot_one(1, jj, 0)
+            if jj > 0:
+                dot_sum(jj - 1)
+            if jj < 4:
+                dot_one(1, jj, 1)
+            if jj > 0:
+                finish(1, jj - 1)
+            if jj < 2:
+                weight_grad(1, 2 * jj)
+                weight_grad(1, 2 * jj + 1)

@@ -27,7 +27,7 @@ G = 2
 NC = E // P
 HALF = D // 2
 NHI = 24
-NPE = 8
+ON_VECTOR = range(8, 16)
 GRID = 2.0**18
 
 
@@ -114,19 +114,19 @@ def tile_qwenextension_v2_v_kernel(
                 )
 
             def x_turn(c):
-                xt = psum.tile([P, 2, 2, G, P], BF16, name="xt", tag="bank")
+                xt = psum.tile([P, 2, G, 2, P], BF16, name="xt", tag="bank")
                 for g in range(G):
                     for j in range(4):
-                        nc.tensor.transpose(xt[:, j % 2, j // 2, g, :], x[g][:, j, P * c : P * (c + 1)], ident_b[:])
+                        nc.tensor.transpose(xt[:, j % 2, g, j // 2, :], x[g][:, j, P * c : P * (c + 1)], ident_b[:])
                 st["xt", c] = xt
 
             def normed_mul(c, l):
                 nt = early.tile([P, 512, 2], BF16, name="nt", tag="nt", bufs=4)
                 nc.vector.scalar_tensor_tensor(
                     nt[:],
-                    st["xt", c][:].rearrange("q e u g p -> q (u g p) e"),
+                    st["xt", c][:].rearrange("q e g u p -> q (g u p) e"),
                     lwls[:, l, c : c + 1],
-                    r_row[l][:].rearrange("q u g p e -> q (u g p) e"),
+                    r_row[l][:].rearrange("q g u p e -> q (g u p) e"),
                     ALU.mult,
                     ALU.mult,
                 )
@@ -137,19 +137,18 @@ def tile_qwenextension_v2_v_kernel(
                 bank = psum.tile([P, G, 2, P], F32, name="nb", tag="bank")
                 for g in range(G):
                     for u in range(2):
-                        w0 = 256 * u + P * g
+                        w0 = 256 * g + P * u
                         nc.tensor.transpose(bank[:, g, u, :], words[:, w0 : w0 + P], ident_f[:])
-                if c % 2 == 0:
-                    st["nint", c // 2, l] = early.tile([P, G, 1024], BF16, name="nint", tag="nint", bufs=4, align_bytes=64)
-                nint = st["nint", c // 2, l]
-                dst = nint[:].bitcast(F32).rearrange("p g (cc e u) -> p g cc e u", cc=2, u=2)[:, :, c % 2]
+                nint = early.tile([P, G, 512], BF16, name="nint", tag="nint", bufs=4, align_bytes=64)
+                dst = nint[:].bitcast(F32).rearrange("p g (e u) -> p g e u", u=2)
                 nc.scalar.copy(dst, bank[:].rearrange("p g u e -> p g e u"))
+                st["nint", c, l] = nint
 
-            def normed_quant(cp, l):
-                cols = slice(2 * P * cp, 2 * P * (cp + 1))
+            def normed_quant(c, l):
+                cols = slice(P * c, P * (c + 1))
                 for g in range(G):
                     nc.vector.quantize_mx(
-                        n_codes[l][g][:, cols].bitcast(E4), n_scales[l][g][:, cols], st["nint", cp, l][:, g, :]
+                        n_codes[l][g][:, cols].bitcast(E4), n_scales[l][g][:, cols], st["nint", c, l][:, g, :]
                     )
 
             def square_sums(u, j):
@@ -162,24 +161,21 @@ def tile_qwenextension_v2_v_kernel(
                     nc.scalar.activation(
                         junk[:], kt[:, j, D * h : D * (h + 1)], ACT.Square, accum_out=ss[:, 4 * j + h : 4 * j + h + 1]
                     )
+                if j == 3:
+                    head_root(u)
+
+            def head_root(u):
+                st["sd", u] = work.tile([P, 16], F32, name="sd", tag="sd")
+                nc.scalar.activation(st["sd", u][:], st["ss", u][:], ACT.Sqrt, bias=EPS, scale=1.0 / D)
 
             def stats(u, part):
                 if part == 0:
-                    for nm in ("var", "rec", "y0", "tmp", "rk", "kap"):
-                        st[nm, u] = work.tile([P, 16], F32, name=nm, tag=nm)
-                var, rec, y0, tmp, rk, kap = [st[nm, u] for nm in ("var", "rec", "y0", "tmp", "rk", "kap")]
-                if part == 0:
-                    nc.vector.tensor_scalar(var[:], st["ss", u][:], 1.0 / D, EPS, ALU.mult, ALU.add)
-                elif part == 1:
-                    nc.vector.reciprocal(rec[:], var[:])
-                    nc.scalar.activation(y0[:], rec[:], ACT.Sqrt)
-                elif part == 2:
-                    nc.vector.tensor_tensor(tmp[:], y0[:], y0[:], ALU.mult)
-                    nc.vector.tensor_scalar(kap[:], rec[:], -1.0 / D, None, ALU.mult)
-                elif part == 3:
-                    nc.vector.scalar_tensor_tensor(tmp[:], tmp[:], -0.5, var[:], ALU.mult, ALU.mult)
+                    st["rk", u] = work.tile([P, 16], F32, name="rk", tag="rk")
+                    nc.vector.reciprocal(st["rk", u][:], st["sd", u][:])
                 else:
-                    nc.vector.scalar_tensor_tensor(rk[:], tmp[:], 1.5, y0[:], ALU.add, ALU.mult)
+                    rk = st["rk", u]
+                    st["kap", u] = work.tile([P, 16], F32, name="kap", tag="kap")
+                    nc.vector.scalar_tensor_tensor(st["kap", u][:], rk[:], -1.0 / D, rk[:], ALU.mult, ALU.mult)
 
             def rope_products(n):
                 u, j = divmod(n, 4)
@@ -198,7 +194,7 @@ def tile_qwenextension_v2_v_kernel(
 
             def rope_sum(n):
                 t = st["t", n]
-                if n >= NPE:
+                if n in ON_VECTOR:
                     return
                 hb = psum.tile([P, H, D], F32, name="hb", tag="hb", bufs=2)
                 nc.tensor.matmul(hb[:], lhsT=ident_f[:], rhs=t[:, :, 0, :], start=True, stop=False)
@@ -208,7 +204,7 @@ def tile_qwenextension_v2_v_kernel(
 
             def rope_add(n):
                 t = st["t", n]
-                if n < NPE:
+                if n not in ON_VECTOR:
                     return
                 for a in range(2):
                     here = t[:, :, 0, HALF * a : HALF * (a + 1)]
@@ -300,7 +296,7 @@ def tile_qwenextension_v2_v_kernel(
                 late = st["late"]
                 toks = slice(P * j, P * (j + 1))
                 if hh == 0:
-                    st["part", j] = late.tile([P, 3], F32, name="part", tag="part", bufs=4)
+                    st["part", j] = late.tile([P, 4], F32, name="part", tag="part", bufs=4)
                     st["negc", j] = late.tile([P, 1], F32, name="negc", tag="negc", bufs=4)
                     st["o1", j] = late.tile([P, E], F32, name="o1", tag="o1", bufs=4)
                 both = psum.tile([P, 4, P], F32, name="both", tag="bank")
@@ -337,44 +333,48 @@ def tile_qwenextension_v2_v_kernel(
                     accum_out=st["part", j][:, hh : hh + 1],
                 )
 
-            def dot_both(g, j):
-                junk = st["late"].tile([P, E], F32, name="junk", tag="junk", bufs=2)
+            def dot_both(g, j, hh):
+                junk = st["late"].tile([P, 512], F32, name="junk", tag="junk", bufs=2)
                 nc.vector.scalar_tensor_tensor(
                     junk[:],
-                    st["o1", j][:],
+                    st["o1", j][:, 512 * hh : 512 * (hh + 1)],
                     alpha[:, 4 * g + j : 4 * g + j + 1],
-                    x[g][:, j, :],
+                    x[g][:, j, 512 * hh : 512 * (hh + 1)],
                     ALU.mult,
                     ALU.mult,
-                    accum_out=st["part", j][:, 2:3],
+                    accum_out=st["part", j][:, 2 + hh : 3 + hh],
                 )
 
             def dot_sum(j):
                 nc.vector.tensor_reduce(st["negc", j][:], st["part", j][:], AX.X, ALU.add)
 
-            def finish(g, j):
+            def finish(g, j, parts=1):
                 o1 = st["o1", j]
-                nc.vector.scalar_tensor_tensor(o1[:], x[g][:, j, :], st["negc", j][:], o1[:], ALU.mult, ALU.add)
-                nc.sync.dma_start(out=o0_hbm[g, j], in_=o1[:])
+                for i in range(parts):
+                    cols = slice(i * E // parts, (i + 1) * E // parts)
+                    nc.vector.scalar_tensor_tensor(
+                        o1[:, cols], x[g][:, j, cols], st["negc", j][:], o1[:, cols], ALU.mult, ALU.add
+                    )
+                    nc.sync.dma_start(out=o0_hbm[g, j][:, cols], in_=o1[:, cols])
 
-            def weight_grad(l, ft):
+            def weight_grad(l, i):
+                ft, hh = divmod(i, 2)
                 rows = slice(P * ft, P * (ft + 1))
-                stage = st["late"].tile([P, E], F32, name="dws", tag="dws", bufs=2)
-                for hh in range(2):
-                    cols = slice(512 * hh, 512 * (hh + 1))
-                    bank = psum.tile([P, 512], F32, name="dw", tag="bank")
-                    for g in range(G):
-                        nc.tensor.matmul_mx(
-                            bank[:],
-                            lhsT=t_codes[l][g][:, rows].bitcast(E5),
-                            lhsT_scale=t_scales[l][g][:, rows],
-                            rhs=n_codes[l][g][:, cols].bitcast(E4),
-                            rhs_scale=n_scales[l][g][:, cols],
-                            start=(g == 0),
-                            stop=(g == G - 1),
-                        )
-                    nc.scalar.copy(stage[:, cols], bank[:])
-                nc.sync.dma_start(out=out_1[l, rows, :], in_=stage[:])
+                cols = slice(512 * hh, 512 * (hh + 1))
+                bank = psum.tile([P, 512], F32, name="dw", tag="bank")
+                for g in range(G):
+                    nc.tensor.matmul_mx(
+                        bank[:],
+                        lhsT=t_codes[l][g][:, rows].bitcast(E5),
+                        lhsT_scale=t_scales[l][g][:, rows],
+                        rhs=n_codes[l][g][:, cols].bitcast(E4),
+                        rhs_scale=n_scales[l][g][:, cols],
+                        start=(g == 0),
+                        stop=(g == G - 1),
+                    )
+                stage = st["late"].tile([P, 512], F32, name="dws", tag="dws", bufs=5)
+                nc.scalar.copy(stage[:], bank[:])
+                nc.sync.dma_start(out=out_1[l, rows, cols], in_=stage[:])
 
             pos = early.tile([P, 4], F32, name="pos")
             nc.gpsimd.iota(pos[:], pattern=[[1, 4]], base=0, channel_multiplier=4, allow_small_or_imprecise_dtypes=True)
@@ -383,7 +383,6 @@ def tile_qwenextension_v2_v_kernel(
             ident_f = keep.tile([P, P], F32, name="ident_f")
             make_identity(nc, ident_f[:])
             ident_b = keep.tile([P, P], BF16, name="ident_b")
-            make_identity(nc, ident_b[:])
 
             rcol = keep.tile([P, L, G, 4], F32, name="rcol")
             nc.scalar.dma_start(
@@ -393,6 +392,7 @@ def tile_qwenextension_v2_v_kernel(
             ls = keep.tile([P, L], BF16, name="ls")
             nc.scalar.dma_start(out=ls[:], in_=layer_scales.partition_broadcast(P))
             nc.scalar.dma_start(out=lwrows[0 : L * NC, :], in_=ln_w.rearrange("l (c p) -> (l c) p", p=P))
+            nc.scalar.copy(ident_b[:], ident_f[:])
             x = [keep.tile([P, 4, E], BF16, name="x%d" % g) for g in range(G)]
 
             def load_x(hh):
@@ -406,8 +406,8 @@ def tile_qwenextension_v2_v_kernel(
             nc.sync.dma_start(
                 out=kw[:].rearrange("p l d -> p (l d)"), in_=kn_w.rearrange("l d -> (l d)").partition_broadcast(P)
             )
-            load_w(0)
             load_g(0)
+            load_w(0)
             load_x(1)
             load_w(1)
             load_k(1)
@@ -440,15 +440,14 @@ def tile_qwenextension_v2_v_kernel(
             beta = keep.tile([P, 8], F32, name="beta")
             lwls = keep.tile([P, L, NC], F32, name="lwls")
             lw_ps = psum.tile([P, P], BF16, name="lw_ps", tag="bank")
-            r_row = [early.tile([P, 2, G, P, 2], F32, name="r_row%d" % l) for l in range(L)]
+            r_row = [early.tile([P, G, 2, P, 2], F32, name="r_row%d" % l) for l in range(L)]
             for l in range(L):
-                for u in range(2):
-                    bank = psum.tile([P, G, 2, P], F32, name="rb", tag="bank")
-                    for g in range(G):
-                        for e2 in range(2):
-                            col = rcol[:, l, g, 2 * u + e2 : 2 * u + e2 + 1]
-                            nc.tensor.transpose(bank[:, g, e2, :], col.to_broadcast([P, P]), ident_f[:])
-                    nc.scalar.copy(r_row[l][:, u], bank[:].rearrange("q g e p -> q g p e"))
+                for g in range(G):
+                    bank = psum.tile([P, 2, 2, P], F32, name="rb", tag="bank")
+                    for j in range(4):
+                        col = rcol[:, l, g, j : j + 1]
+                        nc.tensor.transpose(bank[:, j % 2, j // 2, :], col.to_broadcast([P, P]), ident_f[:])
+                    nc.scalar.copy(r_row[l][:, g], bank[:].rearrange("q e u p -> q u p e"))
             nc.tensor.transpose(lw_ps[:], lwrows[:], ident_b[:])
             nc.vector.tensor_tensor(
                 whole[:],
@@ -508,196 +507,198 @@ def tile_qwenextension_v2_v_kernel(
                     nc.tensor.transpose(bank[:, j, :], col.to_broadcast([P, P]), ident_f[:])
                 nc.scalar.copy(rho_row[:, g, :], bank[:].rearrange("q j p -> q (j p)"))
 
+            def normed_step(i):
+                if i % 2 == 0 and i // 2 + 1 < NC:
+                    x_turn(i // 2 + 1)
+                if 2 <= i < 2 * NC + 2:
+                    normed_turn(*divmod(i - 2, 2))
+
+            def normed_vec(i):
+                if i < 2 * NC:
+                    normed_mul(*divmod(i, 2))
+
+            def normed_q(i):
+                if 4 <= i < 2 * NC + 4:
+                    normed_quant(*divmod(i - 4, 2))
+
             x_turn(0)
-            x_turn(1)
             for j in range(4):
                 square_sums(0, j)
-            normed_mul(0, 0)
-            normed_mul(0, 1)
-            x_turn(2)
-            normed_mul(1, 0)
-            normed_mul(1, 1)
-            stats(0, 0)
-            normed_turn(0, 0)
-            normed_mul(2, 0)
-            stats(0, 1)
-            normed_turn(0, 1)
-            normed_mul(2, 1)
-            x_turn(3)
-            normed_turn(1, 0)
-            normed_turn(1, 1)
-            stats(0, 2)
+            for i in range(6):
+                normed_step(i)
+                if i == 5:
+                    stats(0, 0)
+                normed_vec(i)
             w_group(0)
-            normed_quant(0, 0)
-            stats(0, 3)
-            normed_quant(0, 1)
-            stats(0, 4)
+            normed_q(4)
+            stats(0, 1)
+            normed_q(5)
             for n in range(9):
                 u, j = divmod(n, 4)
-                c = n + 3
+                items = (6 + 2 * n, 7 + 2 * n)
                 rope_products(n)
-                if n < 6:
-                    normed_turn(c - 1, 0)
-                    normed_turn(c - 1, 1)
+                for i in items:
+                    normed_step(i)
+                if n in (1, 2):
+                    dv_turn(0, n - 1)
+                if n in (5, 6):
+                    dv_turn(1, n - 5)
+                if n in (3, 5, 7):
+                    dk_turn((n - 3) // 4, ((n - 3) // 2) % 2)
                 rope_sum(n)
-                if c + 1 < NC:
-                    x_turn(c + 1)
-                if n < 4:
+                if n < 3:
                     square_sums(1, n)
-                elif n < 8:
-                    square_sums(2, n - 4)
-                if n < 7:
-                    w_group(n + 1)
+                    if n == 2:
+                        square_sums(1, 3)
+                elif n < 7:
+                    square_sums(2, n - 3)
+                if j == 3:
+                    stats(u + 1, 0)
                 if n > 0:
                     key_grad(n - 1)
-                if n in (2, 4, 6):
-                    load_w(n // 2 + 1) if n < 6 else None
+                if j == 3:
+                    stats(u + 1, 1)
+                if n < 7:
+                    w_group(n + 1)
+                if n in (2, 4):
+                    load_w(n // 2 + 1)
                 if n == 2:
                     load_k(2)
                 if n == 4:
                     load_g(2)
                     load_k(3)
-                rope_add(n)
-                if n < 8:
-                    w_quant(n)
-                if j == 3:
-                    stats(u + 1, 0)
-                if c < NC:
-                    normed_mul(c, 0)
-                if j == 3:
-                    stats(u + 1, 1)
-                if c < NC:
-                    normed_mul(c, 1)
-                if j == 3:
-                    stats(u + 1, 2)
-                if n in (1, 3, 5):
-                    normed_quant((n + 1) // 2, 0)
-                if j == 3:
-                    stats(u + 1, 3)
-                if n in (1, 3, 5):
-                    normed_quant((n + 1) // 2, 1)
-                if j == 3:
-                    stats(u + 1, 4)
-                if n in (1, 2):
-                    dv_turn(0, n - 1)
-                if n == 3:
-                    feature_quant(0, 1)
-                if n in (2, 4):
-                    dk_turn(0, n // 2 - 1)
-                if n == 5:
-                    feature_quant(0, 0)
-                    dk_group(0)
                     load_dv(2)
-                if n in (5, 6):
-                    dv_turn(1, n - 5)
-                if n == 7:
-                    feature_quant(1, 1)
-                    token_quant(0)
-                    spread_rho(0)
-                    spread_rho(1)
-                if n in (6, 8):
-                    dk_turn(1, n // 2 - 3)
                 if n == 8:
                     load_g(3)
                     load_dv(3)
+                    dk_turn(1, 1)
+                rope_add(n)
+                for i in items:
+                    normed_vec(i)
+                if n < 8:
+                    w_quant(n)
+                normed_q(items[0])
+                if n in (3, 7):
+                    feature_quant(u, 1)
+                normed_q(items[1])
+                if n == 7:
+                    token_quant(0)
+                if n == 5:
+                    dk_group(0)
+                if n == 6:
+                    feature_quant(0, 0)
+                if n == 7:
+                    spread_rho(0)
+                    spread_rho(1)
         st["late"] = ctx.enter_context(tc.tile_pool(name="late", bufs=1))
+
         for n in range(9, 17):
             if n < 16:
                 rope_products(n)
             if n == 9:
                 feature_quant(1, 0)
-                dk_group(1)
-            if n == 9:
                 for jj in range(4):
                     square_sums(3, jj)
+            if n in (9, 10):
+                dv_turn(2, n - 9)
+            if n in (13, 14):
+                dv_turn(3, n - 13)
             if n < 13:
                 for c in (2 * (n - 9), 2 * (n - 9) + 1):
                     dnormed(0, c, 0)
                     dnormed(0, c, 1)
                     dnormed_out(0, c, 1)
-            else:
-                back_turn(0, n - 13, 0)
-                back_turn(0, n - 13, 1)
+                    if n > 10:
+                        back_turn(0, c - 4, 0)
+            if n in (11, 13, 15):
+                dk_turn(2 + (n - 11) // 4, ((n - 11) // 2) % 2)
+            if n in (13, 14):
+                back_turn(0, 2 * (n - 13), 1)
+                back_turn(0, 2 * (n - 13) + 1, 1)
+            if n in (15, 16):
+                for i in range(4 * (n - 15), 4 * (n - 14)):
+                    weight_grad(0, i)
             if n < 16:
                 rope_sum(n)
             if n == 11:
                 stats(3, 0)
             key_grad(n - 1)
+            if n == 16:
+                dk_turn(3, 1)
             if n == 11:
                 stats(3, 1)
             if n < 16:
                 rope_add(n)
-            if n == 11:
-                stats(3, 2)
             if n < 13:
                 dnormed_out(0, 2 * (n - 9), 0)
-                if n == 11:
-                    stats(3, 3)
+                if n > 10:
+                    dot_one(0, 2 * (n - 11), 0)
                 dnormed_out(0, 2 * (n - 9) + 1, 0)
-                if n == 11:
-                    stats(3, 4)
-            else:
-                dot_one(0, n - 13, 0)
-                dot_one(0, n - 13, 1)
-            if n == 10:
-                token_quant(1)
-            if n in (9, 10):
-                dv_turn(2, n - 9)
-            if n == 11:
-                feature_quant(2, 1)
-            if n in (10, 12):
-                dk_turn(2, n // 2 - 5)
-            if n == 13:
-                feature_quant(2, 0)
-                dk_group(2)
+                if n > 10:
+                    dot_one(0, 2 * (n - 11) + 1, 0)
             if n in (13, 14):
-                dv_turn(3, n - 13)
+                dot_one(0, 2 * (n - 13), 1)
+                dot_one(0, 2 * (n - 13) + 1, 1)
+            if n in (9, 13):
+                dk_group((n - 5) // 4)
+            if n in (11, 14):
+                token_quant(1 if n == 11 else 2)
+            if n in (11, 15):
+                feature_quant((n - 3) // 4, 1)
             if n == 14:
-                token_quant(2)
-            if n == 15:
-                feature_quant(3, 1)
-            if n in (14, 16):
-                dk_turn(3, n // 2 - 7)
-            if n == 16:
-                dk_group(3)
-            if n >= 15:
-                weight_grad(0, 2 * (n - 15))
-                weight_grad(0, 2 * (n - 15) + 1)
-        dot_both(0, 0)
-        dot_both(0, 1)
+                feature_quant(2, 0)
+        dot_both(0, 0, 0)
+        dot_both(0, 0, 1)
+        dot_both(0, 1, 0)
         dot_sum(0)
         feature_quant(3, 0)
+        dk_group(3)
         finish(0, 0)
         for c in range(NC):
             dnormed(1, c, 0)
             dnormed(1, c, 1)
             dnormed_out(1, c, 1)
+            if c >= 5:
+                back_turn(1, c - 5, 0)
             if c == 0:
+                dot_both(0, 1, 1)
+                dot_both(0, 2, 0)
                 dot_sum(1)
-                token_quant(3)
             if c == 1:
                 finish(0, 1)
-            if c in (2, 4):
-                dot_both(0, c // 2 + 1)
-            if c in (4, 6):
-                finish(0, c // 2)
+            if c == 2:
+                dot_both(0, 2, 1)
+                token_quant(3)
+                dot_sum(2)
+            if c == 3:
+                finish(0, 2)
+                dot_both(0, 3, 0)
+            if c == 4:
+                dot_both(0, 3, 1)
+            if c == 5:
+                finish(0, 3)
             dnormed_out(1, c, 0)
-            if c in (2, 4):
-                dot_sum(c // 2 + 1)
+            if c == 4:
+                dot_sum(3)
+            if c > 5:
+                dot_one(1, c - 6, 0)
+        back_turn(1, 3, 0)
+        dot_one(1, 2, 0)
         for jj in range(5):
             if jj < 4:
-                back_turn(1, jj, 0)
                 back_turn(1, jj, 1)
+            if jj < 3:
+                for i in range(3 * jj, min(3 * jj + 3, 8)):
+                    weight_grad(1, i)
+            if jj == 0:
+                dot_one(1, 3, 0)
             if jj > 0:
-                dot_both(1, jj - 1)
+                dot_both(1, jj - 1, 1)
             if jj < 4:
-                dot_one(1, jj, 0)
+                dot_both(1, jj, 0)
             if jj > 0:
                 dot_sum(jj - 1)
             if jj < 4:
                 dot_one(1, jj, 1)
             if jj > 0:
-                finish(1, jj - 1)
-            if jj < 2:
-                weight_grad(1, 2 * jj)
-                weight_grad(1, 2 * jj + 1)
+                finish(1, jj - 1, 2 if jj == 4 else 1)

@@ -28,6 +28,8 @@ NC = E // P
 HALF = D // 2
 NHI = 24
 ON_VECTOR = range(8, 16)
+ON_GPSIMD = ()
+TAILG = False
 GRID = 2.0**18
 
 
@@ -82,7 +84,7 @@ def tile_qwenextension_v2_v_kernel(
 
             def load_dv(u):
                 l, g = units[u]
-                dv = work.tile([P, 4, J], BF16, name="dv", tag="dv")
+                dv = work.tile([P, 4, J], BF16, name="dv", tag="dv", bufs=1)
                 for i in range(4):
                     src = grad_out[1, l, 2 * g + i // 2, :, P * (i % 2) : P * (i % 2 + 1), :]
                     nc.sync.dma_start(out=dv[:, i, :].rearrange("q (h d) -> q h d", h=H), in_=src.rearrange("h q d -> q h d"))
@@ -180,7 +182,7 @@ def tile_qwenextension_v2_v_kernel(
             def rope_products(n):
                 u, j = divmod(n, 4)
                 l = units[u][0]
-                t = work.tile([P, H, 2, D], F32, name="t", tag="t", bufs=3)
+                t = work.tile([P, H, 2, D], F32, name="t", tag="t")
                 for h in range(H):
                     nc.vector.scalar_tensor_tensor(
                         t[:, h],
@@ -206,9 +208,10 @@ def tile_qwenextension_v2_v_kernel(
                 t = st["t", n]
                 if n not in ON_VECTOR:
                     return
+                eng = nc.gpsimd if n in ON_GPSIMD else nc.vector
                 for a in range(2):
                     here = t[:, :, 0, HALF * a : HALF * (a + 1)]
-                    nc.vector.tensor_tensor(here, here, t[:, :, 1, HALF * (1 - a) : HALF * (2 - a)], ALU.add)
+                    eng.tensor_tensor(here, here, t[:, :, 1, HALF * (1 - a) : HALF * (2 - a)], ALU.add)
                 st["hb", n] = t[:, :, 0, :]
 
             def key_grad(n):
@@ -283,73 +286,54 @@ def tile_qwenextension_v2_v_kernel(
                     )
                 st["dn", c, l] = bank
 
-            def dnormed_out(g, c, l):
+            def dnormed_out(c, l):
                 at = st["late"].tile([P, 512], F32, name="at", tag="at", bufs=16)
-                bank = st["dn", c, l]
-                if l == 0:
-                    nc.vector.scalar_tensor_tensor(at[:], bank[:], lwls[:, 0, c : c + 1], rho_row[:, g, :], ALU.mult, ALU.mult)
-                else:
-                    nc.scalar.activation(at[:], bank[:], ACT.Copy, scale=lwls[:, 1, c : c + 1])
+                nc.scalar.activation(at[:], st["dn", c, l][:], ACT.Copy, scale=lwls[:, l, c : c + 1])
                 st["at", l, c] = at
 
-            def back_turn(g, j, hh):
+            def back_turn(g, j, hh, l):
                 late = st["late"]
-                toks = slice(P * j, P * (j + 1))
-                if hh == 0:
+                if hh == 0 and l == 1:
                     st["part", j] = late.tile([P, 4], F32, name="part", tag="part", bufs=4)
                     st["negc", j] = late.tile([P, 1], F32, name="negc", tag="negc", bufs=4)
-                    st["o1", j] = late.tile([P, E], F32, name="o1", tag="o1", bufs=4)
-                both = psum.tile([P, 4, P], F32, name="both", tag="bank")
+                bank = psum.tile([P, 4, P], F32, name="back", tag="bank")
                 for cc in range(4):
-                    for l in range(L):
-                        nc.tensor.matmul(
-                            both[:, cc, :],
-                            lhsT=st["at", l, 4 * hh + cc][:, toks],
-                            rhs=ident_f[:],
-                            start=(l == 0),
-                            stop=(l == 1),
-                            is_transpose=True,
-                        )
-                nc.scalar.activation(
-                    st["o1", j][:, 512 * hh : 512 * (hh + 1)],
-                    both[:].rearrange("p c e -> p (c e)"),
-                    ACT.Copy,
-                    scale=rcol[:, 1, g, j : j + 1],
-                )
-                one = psum.tile([P, 4, P], F32, name="one", tag="bank")
-                for cc in range(4):
-                    nc.tensor.transpose(one[:, cc, :], st["at", 1, 4 * hh + cc][:, toks], ident_f[:])
-                st["one", j, hh] = one
+                    nc.tensor.transpose(bank[:, cc, :], st["at", l, 4 * hh + cc][:, P * j : P * (j + 1)], ident_f[:])
+                st["back", j, hh, l] = bank[:].rearrange("p c e -> p (c e)")
+                if l == 1 or g == 0 or TAILG:
+                    if hh == 0:
+                        st["o", j, l] = late.tile([P, E], F32, name="o%d" % l, tag="o%d" % l, bufs=4)
+                    nc.scalar.activation(
+                        st["o", j, l][:, 512 * hh : 512 * (hh + 1)],
+                        st["back", j, hh, l],
+                        ACT.Copy,
+                        scale=rcol[:, l, g, j : j + 1],
+                    )
 
-            def dot_one(g, j, hh):
+            def dot(g, j, hh, l):
                 junk = st["late"].tile([P, 512], F32, name="junk", tag="junk", bufs=2)
                 nc.vector.scalar_tensor_tensor(
                     junk[:],
-                    st["one", j, hh][:].rearrange("p c e -> p (c e)"),
-                    beta[:, 4 * g + j : 4 * g + j + 1],
+                    st["back", j, hh, l],
+                    alpha[:, l, 4 * g + j : 4 * g + j + 1],
                     x[g][:, j, 512 * hh : 512 * (hh + 1)],
                     ALU.mult,
                     ALU.mult,
-                    accum_out=st["part", j][:, hh : hh + 1],
+                    accum_out=st["part", j][:, 2 * l + hh : 2 * l + hh + 1],
                 )
 
-            def dot_both(g, j, hh):
-                junk = st["late"].tile([P, 512], F32, name="junk", tag="junk", bufs=2)
-                nc.vector.scalar_tensor_tensor(
-                    junk[:],
-                    st["o1", j][:, 512 * hh : 512 * (hh + 1)],
-                    alpha[:, 4 * g + j : 4 * g + j + 1],
-                    x[g][:, j, 512 * hh : 512 * (hh + 1)],
-                    ALU.mult,
-                    ALU.mult,
-                    accum_out=st["part", j][:, 2 + hh : 3 + hh],
-                )
+            def add_layers(j, eng):
+                eng.tensor_tensor(st["o", j, 1][:], st["o", j, 1][:], st["o", j, 0][:], ALU.add)
+
+            def add_first_layer(g, j, hh):
+                o1 = st["o", j, 1][:, 512 * hh : 512 * (hh + 1)]
+                nc.vector.scalar_tensor_tensor(o1, st["back", j, hh, 0], rcol[:, 0, g, j : j + 1], o1, ALU.mult, ALU.add)
 
             def dot_sum(j):
                 nc.vector.tensor_reduce(st["negc", j][:], st["part", j][:], AX.X, ALU.add)
 
             def finish(g, j, parts=1):
-                o1 = st["o1", j]
+                o1 = st["o", j, 1]
                 for i in range(parts):
                     cols = slice(i * E // parts, (i + 1) * E // parts)
                     nc.vector.scalar_tensor_tensor(
@@ -372,7 +356,7 @@ def tile_qwenextension_v2_v_kernel(
                         start=(g == 0),
                         stop=(g == G - 1),
                     )
-                stage = st["late"].tile([P, 512], F32, name="dws", tag="dws", bufs=5)
+                stage = st["late"].tile([P, 512], F32, name="dws", tag="dws", bufs=4)
                 nc.scalar.copy(stage[:], bank[:])
                 nc.sync.dma_start(out=out_1[l, rows, cols], in_=stage[:])
 
@@ -413,7 +397,6 @@ def tile_qwenextension_v2_v_kernel(
             load_k(1)
             load_dv(0)
             load_g(1)
-            load_dv(1)
 
             onezero = early.tile([P, 2], F32, name="onezero")
             nc.vector.memset(onezero[:, 0:1], 1.0)
@@ -435,9 +418,7 @@ def tile_qwenextension_v2_v_kernel(
             nphase = early.tile([P, 2, 4, HALF], F32, name="nphase")
             rflat = rcol[:].rearrange("p l g j -> p l (g j)")
             rsq = early.tile([P, L, 8], F32, name="rsq")
-            rho = early.tile([P, 8], F32, name="rho")
-            alpha = keep.tile([P, 8], F32, name="alpha")
-            beta = keep.tile([P, 8], F32, name="beta")
+            alpha = keep.tile([P, L, 8], F32, name="alpha")
             lwls = keep.tile([P, L, NC], F32, name="lwls")
             lw_ps = psum.tile([P, P], BF16, name="lw_ps", tag="bank")
             r_row = [early.tile([P, G, 2, P, 2], F32, name="r_row%d" % l) for l in range(L)]
@@ -462,11 +443,9 @@ def tile_qwenextension_v2_v_kernel(
                 ALU.mult,
             )
             nc.vector.tensor_copy(whole_i[:], whole[:])
-            nc.vector.reciprocal(rho[:], rflat[:, 1, :])
             nc.vector.tensor_tensor(whole[:], whole[:], whole_i[:], ALU.subtract)
             nc.vector.tensor_tensor(rsq[:], rflat, ls[:].unsqueeze(2).to_broadcast([P, L, 8]), ALU.mult)
             nc.vector.tensor_tensor(phase[:, 0, :, 0:NHI], phase[:, 0, :, 0:NHI], whole[:], ALU.add)
-            nc.vector.tensor_tensor(rho[:], rho[:], rflat[:, 0, :], ALU.mult)
             nc.vector.tensor_scalar(phase[:, 1], phase[:, 0], 0.25, None, ALU.add)
             nc.vector.tensor_tensor(rsq[:], rsq[:], rsq[:], ALU.mult)
             flat = "p a j i -> p (a j i)"
@@ -475,9 +454,7 @@ def tile_qwenextension_v2_v_kernel(
             )
             for l in range(L):
                 nc.vector.tensor_scalar(lwls[:, l, :], lw_ps[:, l * NC : (l + 1) * NC], ls[:, l : l + 1], None, ALU.mult)
-            nc.vector.tensor_tensor(beta[:], rsq[:, 0, :], rsq[:, 1, :], ALU.subtract)
-            nc.vector.tensor_scalar(alpha[:], rsq[:, 0, :], -1.0 / E, None, ALU.mult)
-            nc.vector.scalar_tensor_tensor(beta[:], beta[:], 1.0 / E, rflat[:, 1, :], ALU.mult, ALU.mult)
+            nc.vector.scalar_tensor_tensor(alpha[:], rsq[:], -1.0 / E, rflat, ALU.mult, ALU.mult)
             cos_t = early.tile([P, 4, HALF], F32, name="cos_t")
             sin_t = early.tile([P, 4, 2, HALF], F32, name="sin_t")
             nc.scalar.activation(cos_t[:], nphase[:, 1], ACT.Sin, scale=-2 * math.pi)
@@ -498,15 +475,6 @@ def tile_qwenextension_v2_v_kernel(
                         kw[:, l, HALF * (1 - a) : HALF * (2 - a)].unsqueeze(1).to_broadcast([P, 4, HALF]),
                         ALU.mult,
                     )
-            rho_row = keep.tile([P, G, 4 * P], F32, name="rho_row")
-
-            def spread_rho(g):
-                bank = psum.tile([P, 4, P], F32, name="rhob", tag="bank")
-                for j in range(4):
-                    col = rho[:, 4 * g + j : 4 * g + j + 1]
-                    nc.tensor.transpose(bank[:, j, :], col.to_broadcast([P, P]), ident_f[:])
-                nc.scalar.copy(rho_row[:, g, :], bank[:].rearrange("q j p -> q (j p)"))
-
             def normed_step(i):
                 if i % 2 == 0 and i // 2 + 1 < NC:
                     x_turn(i // 2 + 1)
@@ -552,6 +520,9 @@ def tile_qwenextension_v2_v_kernel(
                         square_sums(1, 3)
                 elif n < 7:
                     square_sums(2, n - 3)
+                else:
+                    square_sums(3, 2 * (n - 7))
+                    square_sums(3, 2 * (n - 7) + 1)
                 if j == 3:
                     stats(u + 1, 0)
                 if n > 0:
@@ -562,16 +533,17 @@ def tile_qwenextension_v2_v_kernel(
                     w_group(n + 1)
                 if n in (2, 4):
                     load_w(n // 2 + 1)
+                if n in (2, 6):
+                    load_dv(n // 4 + 1)
                 if n == 2:
                     load_k(2)
                 if n == 4:
                     load_g(2)
                     load_k(3)
-                    load_dv(2)
                 if n == 8:
                     load_g(3)
-                    load_dv(3)
                     dk_turn(1, 1)
+                    dk_group(1)
                 rope_add(n)
                 for i in items:
                     normed_vec(i)
@@ -587,118 +559,109 @@ def tile_qwenextension_v2_v_kernel(
                     dk_group(0)
                 if n == 6:
                     feature_quant(0, 0)
-                if n == 7:
-                    spread_rho(0)
-                    spread_rho(1)
         st["late"] = ctx.enter_context(tc.tile_pool(name="late", bufs=1))
+
+        def turn_pair(g, j, hh):
+            back_turn(g, j, hh, 1)
+            back_turn(g, j, hh, 0)
+            if g == 1 and TAILG:
+                add_layers(j, hh, nc.gpsimd)
+
+        def dot_pair(g, j, hh):
+            dot(g, j, hh, 1)
+            dot(g, j, hh, 0)
+            if g == 1 and not TAILG:
+                add_first_layer(g, j, hh)
 
         for n in range(9, 17):
             if n < 16:
                 rope_products(n)
+                rope_sum(n)
+            if n in ON_GPSIMD:
+                rope_add(n)
+                if n > 11:
+                    add_layers(n - 12, 0, nc.gpsimd)
+            if n in (12, 13, 14, 15):
+                hh, jp = divmod(n - 12, 2)
+                dot_pair(0, 2 * jp, hh)
+                dot_pair(0, 2 * jp + 1, hh)
             if n == 9:
                 feature_quant(1, 0)
-                for jj in range(4):
-                    square_sums(3, jj)
             if n in (9, 10):
                 dv_turn(2, n - 9)
+            if n == 10:
+                load_dv(3)
             if n in (13, 14):
                 dv_turn(3, n - 13)
-            if n < 13:
-                for c in (2 * (n - 9), 2 * (n - 9) + 1):
-                    dnormed(0, c, 0)
-                    dnormed(0, c, 1)
-                    dnormed_out(0, c, 1)
-                    if n > 10:
-                        back_turn(0, c - 4, 0)
             if n in (11, 13, 15):
                 dk_turn(2 + (n - 11) // 4, ((n - 11) // 2) % 2)
-            if n in (13, 14):
-                back_turn(0, 2 * (n - 13), 1)
-                back_turn(0, 2 * (n - 13) + 1, 1)
-            if n in (15, 16):
-                for i in range(4 * (n - 15), 4 * (n - 14)):
+            if n < 13:
+                for c in (2 * (n - 9), 2 * (n - 9) + 1):
+                    for l in range(L):
+                        dnormed(0, c, l)
+                        dnormed_out(c, l)
+            if n in (11, 12, 13, 14):
+                hh, jp = divmod(n - 11, 2)
+                turn_pair(0, 2 * jp, hh)
+                turn_pair(0, 2 * jp + 1, hh)
+            if n == 15:
+                for i in range(8):
                     weight_grad(0, i)
-            if n < 16:
-                rope_sum(n)
+            if n == 16:
+                for c in range(4):
+                    dnormed(1, c, 0)
+                    dnormed_out(c, 0)
             if n == 11:
                 stats(3, 0)
             key_grad(n - 1)
             if n == 16:
                 dk_turn(3, 1)
+                dk_group(3)
             if n == 11:
                 stats(3, 1)
-            if n < 16:
+            if n < 16 and n not in ON_GPSIMD:
                 rope_add(n)
-            if n < 13:
-                dnormed_out(0, 2 * (n - 9), 0)
-                if n > 10:
-                    dot_one(0, 2 * (n - 11), 0)
-                dnormed_out(0, 2 * (n - 9) + 1, 0)
-                if n > 10:
-                    dot_one(0, 2 * (n - 11) + 1, 0)
-            if n in (13, 14):
-                dot_one(0, 2 * (n - 13), 1)
-                dot_one(0, 2 * (n - 13) + 1, 1)
-            if n in (9, 13):
-                dk_group((n - 5) // 4)
-            if n in (11, 14):
-                token_quant(1 if n == 11 else 2)
+            if n == 13:
+                dk_group(2)
+            if n == 10:
+                token_quant(1)
             if n in (11, 15):
                 feature_quant((n - 3) // 4, 1)
             if n == 14:
                 feature_quant(2, 0)
-        dot_both(0, 0, 0)
-        dot_both(0, 0, 1)
-        dot_both(0, 1, 0)
-        dot_sum(0)
+                token_quant(2)
+            if n == 16:
+                for jj in range(4):
+                    dot_sum(jj)
+        add_layers(0, nc.vector)
+        add_layers(1, nc.vector)
         feature_quant(3, 0)
-        dk_group(3)
         finish(0, 0)
-        for c in range(NC):
-            dnormed(1, c, 0)
+        for c in range(4):
             dnormed(1, c, 1)
-            dnormed_out(1, c, 1)
-            if c >= 5:
-                back_turn(1, c - 5, 0)
-            if c == 0:
-                dot_both(0, 1, 1)
-                dot_both(0, 2, 0)
-                dot_sum(1)
-            if c == 1:
-                finish(0, 1)
-            if c == 2:
-                dot_both(0, 2, 1)
-                token_quant(3)
-                dot_sum(2)
-            if c == 3:
-                finish(0, 2)
-                dot_both(0, 3, 0)
+            dnormed_out(c, 1)
+        finish(0, 1)
+        add_layers(2, nc.vector)
+        add_layers(3, nc.vector)
+        token_quant(3)
+        finish(0, 2)
+        for c in range(4, NC):
+            turn_pair(1, c - 4, 0)
+            for l in range(L):
+                dnormed(1, c, l)
+                dnormed_out(c, l)
             if c == 4:
-                dot_both(0, 3, 1)
-            if c == 5:
                 finish(0, 3)
-            dnormed_out(1, c, 0)
-            if c == 4:
-                dot_sum(3)
-            if c > 5:
-                dot_one(1, c - 6, 0)
-        back_turn(1, 3, 0)
-        dot_one(1, 2, 0)
+            dot_pair(1, c - 4, 0)
         for jj in range(5):
             if jj < 4:
-                back_turn(1, jj, 1)
+                turn_pair(1, jj, 1)
             if jj < 3:
                 for i in range(3 * jj, min(3 * jj + 3, 8)):
                     weight_grad(1, i)
-            if jj == 0:
-                dot_one(1, 3, 0)
-            if jj > 0:
-                dot_both(1, jj - 1, 1)
-            if jj < 4:
-                dot_both(1, jj, 0)
             if jj > 0:
                 dot_sum(jj - 1)
             if jj < 4:
-                dot_one(1, jj, 1)
+                dot_pair(1, jj, 1)
             if jj > 0:
-                finish(1, jj - 1, 2 if jj == 4 else 1)
+                finish(1, jj - 1, 4 if jj == 4 else 1)

import math
from contextlib import ExitStack

import concourse.mybir as mybir
from concourse.masks import make_identity

L, B, S, E, H, D = 2, 4, 256, 1024, 4, 128
T = B * S
J = H * D
THETA = 1000000.0
EPS = 1e-6
FLOPS = 2 * L * T * (2 * J) * E + 2 * L * J * T * E

F32 = mybir.dt.float32
BF16 = mybir.dt.bfloat16
I32 = mybir.dt.int32
U32 = mybir.dt.uint32
U8 = mybir.dt.uint8
E4 = mybir.dt.float8_e4m3fn_x4
E5 = mybir.dt.float8_e5m2_x4
ALU = mybir.AluOpType
ACT = mybir.ActivationFunctionType
AX = mybir.AxisListType

P = 128
G = 2
NC = E // P
HALF = D // 2
NHI = 24
ON_VECTOR = range(8, 16)
ON_GPSIMD = ()
TAILG = False
GRID = 2.0**18


def tile_qwenextension_v2_v_kernel(
    tc, image_context, layer_scales, ln_w, Wk, Wv, kn_w, k, inv_rms, grad_out, out_0, out_1
):
    nc = tc.nc
    x_hbm = image_context.rearrange("b s e -> (b s) e").rearrange("(g p j) e -> g p j e", g=G, j=4)
    o0_hbm = out_0.rearrange("b s e -> (b s) e").rearrange("(g p j) e -> g j p e", g=G, j=4)
    k_hbm = k.rearrange("l b s f -> l (b s) f").rearrange("l (g p j) f -> l g p (j f)", g=G, j=4)
    w_hbm = [Wk, Wv]

    with ExitStack() as ctx:
        ctx.enter_context(tc.manual_schedule())
        keep = ctx.enter_context(tc.tile_pool(name="keep", bufs=1))
        work = ctx.enter_context(tc.tile_pool(name="work", bufs=2))
        psum = ctx.enter_context(tc.psum_pool(name="psum", bufs=6))
        with tc.tile_pool(name="early", bufs=1) as early:

            n_codes = [[keep.tile([P, E], U32, name="nc%d%d" % (l, g), align_bytes=64) for g in range(G)] for l in range(L)]
            n_scales = [[keep.tile([P, E], U8, name="ns%d%d" % (l, g), align_bytes=64) for g in range(G)] for l in range(L)]
            w_codes = [[keep.tile([P, E], U32, name="wc%d%d" % (l, m), align_bytes=64) for m in range(2)] for l in range(L)]
            w_scales = [[keep.tile([P, E], U8, name="ws%d%d" % (l, m), align_bytes=64) for m in range(2)] for l in range(L)]
            t_codes = [[keep.tile([P, J], U32, name="tc%d%d" % (l, g), align_bytes=64) for g in range(G)] for l in range(L)]
            t_scales = [[keep.tile([P, J], U8, name="ts%d%d" % (l, g), align_bytes=64) for g in range(G)] for l in range(L)]
            f_codes = {}
            f_scales = {}
            for l in range(L):
                for g in range(G):
                    for m in range(2):
                        f_codes[l, g, m] = keep.tile([P, 512], U32, name="fc%d%d%d" % (l, g, m), align_bytes=64)
                        f_scales[l, g, m] = keep.tile([P, 512], U8, name="fs%d%d%d" % (l, g, m), align_bytes=64)

            st = {}
            units = [(0, 0), (1, 0), (0, 1), (1, 1)]

            def load_k(u):
                l, g = units[u]
                kt = work.tile([P, 4, J], F32, name="kt", tag="kt", bufs=3)
                nc.sync.dma_start(out=kt[:].rearrange("p j f -> p (j f)"), in_=k_hbm[l, g])
                st["k", u] = kt

            def load_g(u):
                l, g = units[u]
                gt = work.tile([P, H, 4, D], BF16, name="gt", tag="gt")
                for bb in range(2):
                    nc.sync.dma_start(
                        out=gt[64 * bb : 64 * (bb + 1)].rearrange("q h j d -> q h (j d)"),
                        in_=grad_out[0, l, 2 * g + bb].rearrange("h (q j) d -> q h (j d)", j=4),
                    )
                st["g", u] = gt

            def load_dv(u):
                l, g = units[u]
                dv = work.tile([P, 4, J], BF16, name="dv", tag="dv", bufs=1)
                for i in range(4):
                    src = grad_out[1, l, 2 * g + i // 2, :, P * (i % 2) : P * (i % 2 + 1), :]
                    nc.sync.dma_start(out=dv[:, i, :].rearrange("q (h d) -> q h d", h=H), in_=src.rearrange("h q d -> q h d"))
                st["dv", u] = dv

            def load_w(w):
                l, m = divmod(w, 2)
                raw = early.tile([P, 4, E], BF16, name="wraw", tag="wraw", bufs=2)
                nc.sync.dma_start(
                    out=raw[:].rearrange("p j e -> p (j e)"), in_=w_hbm[m][l].rearrange("(p j) e -> p (j e)", j=4)
                )
                st["w", w] = raw

            def interleave(dst, src):
                nc.scalar.copy(dst.rearrange("p (c i) t -> p c t i", i=4), src.rearrange("p t (c i) -> p c t i", i=4))

            def w_group(i):
                w, hh = divmod(i, 2)
                grouped = early.tile([P, 512, 4], BF16, name="wint", tag="wint", bufs=2, align_bytes=64)
                interleave(grouped[:], st["w", w][:, :, 512 * hh : 512 * (hh + 1)])
                st["wint", i] = grouped

            def w_quant(i):
                w, hh = divmod(i, 2)
                l, m = divmod(w, 2)
                cols = slice(512 * hh, 512 * (hh + 1))
                nc.vector.quantize_mx(
                    w_codes[l][m][:, cols].bitcast(E4), w_scales[l][m][:, cols], st["wint", i][:].rearrange("p e t -> p (e t)")
                )

            def x_turn(c):
                xt = psum.tile([P, 2, G, 2, P], BF16, name="xt", tag="bank")
                for g in range(G):
                    for j in range(4):
                        nc.tensor.transpose(xt[:, j % 2, g, j // 2, :], x[g][:, j, P * c : P * (c + 1)], ident_b[:])
                st["xt", c] = xt

            def normed_mul(c, l):
                nt = early.tile([P, 512, 2], BF16, name="nt", tag="nt", bufs=4)
                nc.vector.scalar_tensor_tensor(
                    nt[:],
                    st["xt", c][:].rearrange("q e g u p -> q (g u p) e"),
                    lwls[:, l, c : c + 1],
                    r_row[l][:].rearrange("q g u p e -> q (g u p) e"),
                    ALU.mult,
                    ALU.mult,
                )
                st["nt", c, l] = nt

            def normed_turn(c, l):
                words = st["nt", c, l][:].rearrange("q w e -> q (w e)").bitcast(F32)
                bank = psum.tile([P, G, 2, P], F32, name="nb", tag="bank")
                for g in range(G):
                    for u in range(2):
                        w0 = 256 * g + P * u
                        nc.tensor.transpose(bank[:, g, u, :], words[:, w0 : w0 + P], ident_f[:])
                nint = early.tile([P, G, 512], BF16, name="nint", tag="nint", bufs=4, align_bytes=64)
                dst = nint[:].bitcast(F32).rearrange("p g (e u) -> p g e u", u=2)
                nc.scalar.copy(dst, bank[:].rearrange("p g u e -> p g e u"))
                st["nint", c, l] = nint

            def normed_quant(c, l):
                cols = slice(P * c, P * (c + 1))
                for g in range(G):
                    nc.vector.quantize_mx(
                        n_codes[l][g][:, cols].bitcast(E4), n_scales[l][g][:, cols], st["nint", c, l][:, g, :]
                    )

            def square_sums(u, j):
                kt = st["k", u]
                if j == 0:
                    st["ss", u] = work.tile([P, 16], F32, name="ss", tag="ss")
                ss = st["ss", u]
                for h in range(H):
                    junk = work.tile([P, D], F32, name="sqj", tag="sqj")
                    nc.scalar.activation(
                        junk[:], kt[:, j, D * h : D * (h + 1)], ACT.Square, accum_out=ss[:, 4 * j + h : 4 * j + h + 1]
                    )
                if j == 3:
                    head_root(u)

            def head_root(u):
                st["sd", u] = work.tile([P, 16], F32, name="sd", tag="sd")
                nc.scalar.activation(st["sd", u][:], st["ss", u][:], ACT.Sqrt, bias=EPS, scale=1.0 / D)

            def stats(u, part):
                if part == 0:
                    st["rk", u] = work.tile([P, 16], F32, name="rk", tag="rk")
                    nc.vector.reciprocal(st["rk", u][:], st["sd", u][:])
                else:
                    rk = st["rk", u]
                    st["kap", u] = work.tile([P, 16], F32, name="kap", tag="kap")
                    nc.vector.scalar_tensor_tensor(st["kap", u][:], rk[:], -1.0 / D, rk[:], ALU.mult, ALU.mult)

            def rope_products(n):
                u, j = divmod(n, 4)
                l = units[u][0]
                t = work.tile([P, H, 2, D], F32, name="t", tag="t")
                for h in range(H):
                    nc.vector.scalar_tensor_tensor(
                        t[:, h],
                        st["g", u][:, h, j].unsqueeze(1).to_broadcast([P, 2, D]),
                        st["rk", u][:, 4 * j + h : 4 * j + h + 1],
                        rope[l][:, j],
                        ALU.mult,
                        ALU.mult,
                    )
                st["t", n] = t

            def rope_sum(n):
                t = st["t", n]
                if n in ON_VECTOR:
                    return
                hb = psum.tile([P, H, D], F32, name="hb", tag="hb", bufs=2)
                nc.tensor.matmul(hb[:], lhsT=ident_f[:], rhs=t[:, :, 0, :], start=True, stop=False)
                nc.tensor.matmul(hb[:, :, 0:HALF], lhsT=ident_f[:], rhs=t[:, :, 1, HALF:D], start=False, stop=False)
                nc.tensor.matmul(hb[:, :, HALF:D], lhsT=ident_f[:], rhs=t[:, :, 1, 0:HALF], start=False, stop=True)
                st["hb", n] = hb

            def rope_add(n):
                t = st["t", n]
                if n not in ON_VECTOR:
                    return
                eng = nc.gpsimd if n in ON_GPSIMD else nc.vector
                for a in range(2):
                    here = t[:, :, 0, HALF * a : HALF * (a + 1)]
                    eng.tensor_tensor(here, here, t[:, :, 1, HALF * (1 - a) : HALF * (2 - a)], ALU.add)
                st["hb", n] = t[:, :, 0, :]

            def key_grad(n):
                u, j = divmod(n, 4)
                if j == 0:
                    st["dk", u] = work.tile([P, 4, J], BF16, name="dk", tag="dk")
                    st["coef", u] = work.tile([P, 16], F32, name="coef", tag="coef")
                kt, kap, dk, coef, t, hb = st["k", u], st["kap", u], st["dk", u], st["coef", u], st["t", n], st["hb", n]
                for h in range(H):
                    s = slice(4 * j + h, 4 * j + h + 1)
                    kh = kt[:, j, D * h : D * (h + 1)]
                    nc.vector.scalar_tensor_tensor(
                        t[:, h, 1], hb[:, h], kap[:, s], kh, ALU.mult, ALU.mult, accum_out=coef[:, s]
                    )
                for h in range(H):
                    s = slice(4 * j + h, 4 * j + h + 1)
                    kh = kt[:, j, D * h : D * (h + 1)]
                    nc.vector.scalar_tensor_tensor(dk[:, j, D * h : D * (h + 1)], kh, coef[:, s], hb[:, h], ALU.mult, ALU.add)

            def dk_turn(u, jp):
                if jp == 0:
                    st["dt", u, 0] = work.tile([P, 4, P, 4], BF16, name="dt", tag="dt", align_bytes=64)
                dtw = st["dt", u, 0][:].rearrange("p j r t -> p (j r t)").bitcast(F32).rearrange("p (j r u) -> p j r u", j=4, u=2)
                bank = psum.tile([P, 2, 2, P], F32, name="kb", tag="bank")
                for jj in range(2):
                    words = st["dk", u][:, 2 * jp + jj, :].bitcast(F32)
                    for v in range(2):
                        nc.tensor.transpose(bank[:, jj, v, :], words[:, v : 256 : 2], ident_f[:])
                nc.scalar.copy(dtw[:, 2 * jp : 2 * jp + 2], bank[:].rearrange("p j u r -> p j r u"))

            def dv_turn(u, ip):
                if ip == 0:
                    st["dt", u, 1] = work.tile([P, 4, P, 4], BF16, name="dt", tag="dt", align_bytes=64)
                dtw = st["dt", u, 1][:].rearrange("p j r t -> p (j r t)").bitcast(F32)
                dtw = dtw.rearrange("p (j ip ii q u) -> p j ip ii q u", j=4, ip=2, ii=2, u=2)
                bank = psum.tile([P, 2, 2, P], F32, name="vb", tag="bank")
                for ii in range(2):
                    words = st["dv", u][:, 2 * ip + ii, :].bitcast(F32)
                    for v in range(2):
                        nc.tensor.transpose(bank[:, ii, v, :], words[:, v : 256 : 2], ident_f[:])
                nc.scalar.copy(dtw[:, :, ip], bank[:].rearrange("p ii u (q j) -> p j ii q u", j=4))

            def feature_quant(u, m):
                l, g = units[u]
                nc.vector.quantize_mx(
                    f_codes[l, g, m][:].bitcast(E5), f_scales[l, g, m][:], st["dt", u, m][:].rearrange("p j r t -> p (j r t)")
                )

            def dk_group(u):
                grouped = work.tile([P, J, 4], BF16, name="dki", tag="dki", bufs=1, align_bytes=64)
                interleave(grouped[:], st["dk", u][:])
                st["dki", u] = grouped

            def token_quant(u):
                l, g = units[u]
                nc.vector.quantize_mx(
                    t_codes[l][g][:].bitcast(E5), t_scales[l][g][:], st["dki", u][:].rearrange("p f t -> p (f t)")
                )

            def dnormed(g, c, l):
                cols = slice(P * c, P * (c + 1))
                bank = psum.tile([P, 512], F32, name="dn", tag="bank")
                for m in range(2):
                    nc.tensor.matmul_mx(
                        bank[:],
                        lhsT=w_codes[l][m][:, cols].bitcast(E4),
                        lhsT_scale=w_scales[l][m][:, cols],
                        rhs=f_codes[l, g, m][:].bitcast(E5),
                        rhs_scale=f_scales[l, g, m][:],
                        start=(m == 0),
                        stop=(m == 1),
                    )
                st["dn", c, l] = bank

            def dnormed_out(c, l):
                at = st["late"].tile([P, 512], F32, name="at", tag="at", bufs=16)
                nc.scalar.activation(at[:], st["dn", c, l][:], ACT.Copy, scale=lwls[:, l, c : c + 1])
                st["at", l, c] = at

            def back_turn(g, j, hh, l):
                late = st["late"]
                if hh == 0 and l == 1:
                    st["part", j] = late.tile([P, 4], F32, name="part", tag="part", bufs=4)
                    st["negc", j] = late.tile([P, 1], F32, name="negc", tag="negc", bufs=4)
                bank = psum.tile([P, 4, P], F32, name="back", tag="bank")
                for cc in range(4):
                    nc.tensor.transpose(bank[:, cc, :], st["at", l, 4 * hh + cc][:, P * j : P * (j + 1)], ident_f[:])
                st["back", j, hh, l] = bank[:].rearrange("p c e -> p (c e)")
                if l == 1 or g == 0 or TAILG:
                    if hh == 0:
                        st["o", j, l] = late.tile([P, E], F32, name="o%d" % l, tag="o%d" % l, bufs=4)
                    nc.scalar.activation(
                        st["o", j, l][:, 512 * hh : 512 * (hh + 1)],
                        st["back", j, hh, l],
                        ACT.Copy,
                        scale=rcol[:, l, g, j : j + 1],
                    )

            def dot(g, j, hh, l):
                junk = st["late"].tile([P, 512], F32, name="junk", tag="junk", bufs=2)
                nc.vector.scalar_tensor_tensor(
                    junk[:],
                    st["back", j, hh, l],
                    alpha[:, l, 4 * g + j : 4 * g + j + 1],
                    x[g][:, j, 512 * hh : 512 * (hh + 1)],
                    ALU.mult,
                    ALU.mult,
                    accum_out=st["part", j][:, 2 * l + hh : 2 * l + hh + 1],
                )

            def add_layers(j, eng):
                eng.tensor_tensor(st["o", j, 1][:], st["o", j, 1][:], st["o", j, 0][:], ALU.add)

            def add_first_layer(g, j, hh):
                o1 = st["o", j, 1][:, 512 * hh : 512 * (hh + 1)]
                nc.vector.scalar_tensor_tensor(o1, st["back", j, hh, 0], rcol[:, 0, g, j : j + 1], o1, ALU.mult, ALU.add)

            def dot_sum(j):
                nc.vector.tensor_reduce(st["negc", j][:], st["part", j][:], AX.X, ALU.add)

            def finish(g, j, parts=1):
                o1 = st["o", j, 1]
                for i in range(parts):
                    cols = slice(i * E // parts, (i + 1) * E // parts)
                    nc.vector.scalar_tensor_tensor(
                        o1[:, cols], x[g][:, j, cols], st["negc", j][:], o1[:, cols], ALU.mult, ALU.add
                    )
                    nc.sync.dma_start(out=o0_hbm[g, j][:, cols], in_=o1[:, cols])

            def weight_grad(l, i):
                ft, hh = divmod(i, 2)
                rows = slice(P * ft, P * (ft + 1))
                cols = slice(512 * hh, 512 * (hh + 1))
                bank = psum.tile([P, 512], F32, name="dw", tag="bank")
                for g in range(G):
                    nc.tensor.matmul_mx(
                        bank[:],
                        lhsT=t_codes[l][g][:, rows].bitcast(E5),
                        lhsT_scale=t_scales[l][g][:, rows],
                        rhs=n_codes[l][g][:, cols].bitcast(E4),
                        rhs_scale=n_scales[l][g][:, cols],
                        start=(g == 0),
                        stop=(g == G - 1),
                    )
                stage = st["late"].tile([P, 512], F32, name="dws", tag="dws", bufs=4)
                nc.scalar.copy(stage[:], bank[:])
                nc.sync.dma_start(out=out_1[l, rows, cols], in_=stage[:])

            pos = early.tile([P, 4], F32, name="pos")
            nc.gpsimd.iota(pos[:], pattern=[[1, 4]], base=0, channel_multiplier=4, allow_small_or_imprecise_dtypes=True)
            lwrows = early.tile([P, P], BF16, name="lwrows")
            nc.gpsimd.memset(lwrows[:], 0.0)
            ident_f = keep.tile([P, P], F32, name="ident_f")
            make_identity(nc, ident_f[:])
            ident_b = keep.tile([P, P], BF16, name="ident_b")

            rcol = keep.tile([P, L, G, 4], F32, name="rcol")
            nc.scalar.dma_start(
                out=rcol[:].rearrange("p l g j -> p (l g) j"),
                in_=inv_rms.rearrange("l b s -> (l b s)").rearrange("(m p j) -> p m j", p=P, j=4),
            )
            ls = keep.tile([P, L], BF16, name="ls")
            nc.scalar.dma_start(out=ls[:], in_=layer_scales.partition_broadcast(P))
            nc.scalar.dma_start(out=lwrows[0 : L * NC, :], in_=ln_w.rearrange("l (c p) -> (l c) p", p=P))
            nc.scalar.copy(ident_b[:], ident_f[:])
            x = [keep.tile([P, 4, E], BF16, name="x%d" % g) for g in range(G)]

            def load_x(hh):
                for g in range(G):
                    cols = slice(512 * hh, 512 * (hh + 1))
                    nc.sync.dma_start(out=x[g][:, :, cols], in_=x_hbm[g][:, :, cols])

            load_x(0)
            load_k(0)
            kw = early.tile([P, L, D], BF16, name="kw")
            nc.sync.dma_start(
                out=kw[:].rearrange("p l d -> p (l d)"), in_=kn_w.rearrange("l d -> (l d)").partition_broadcast(P)
            )
            load_g(0)
            load_w(0)
            load_x(1)
            load_w(1)
            load_k(1)
            load_dv(0)
            load_g(1)

            onezero = early.tile([P, 2], F32, name="onezero")
            nc.vector.memset(onezero[:, 0:1], 1.0)
            nc.vector.memset(onezero[:, 1:2], 0.0)
            wrap = early.tile([P, 4], F32, name="wrap")
            freq = early.tile([P, 2, HALF], F32, name="freq")
            turns = [THETA ** (-i / HALF) / (2 * math.pi) for i in range(HALF)]
            for i in range(NHI):
                hi = int(turns[i] * GRID) / GRID
                nc.vector.tensor_scalar(freq[:, :, i], onezero[:], hi, turns[i] - hi, ALU.min, ALU.max)
            nc.vector.tensor_scalar(wrap[:], pos[:], float(S), -float(S), ALU.is_ge, ALU.mult)
            for i in range(NHI, HALF, 2):
                nc.vector.tensor_scalar(freq[:, 1, i : i + 2], onezero[:], turns[i], turns[i + 1], ALU.min, ALU.max)
                if i == NHI:
                    nc.vector.tensor_tensor(pos[:], pos[:], wrap[:], ALU.add)
            whole = early.tile([P, 4, NHI], F32, name="whole")
            whole_i = early.tile([P, 4, NHI], I32, name="whole_i")
            phase = early.tile([P, 2, 4, HALF], F32, name="phase")
            nphase = early.tile([P, 2, 4, HALF], F32, name="nphase")
            rflat = rcol[:].rearrange("p l g j -> p l (g j)")
            rsq = early.tile([P, L, 8], F32, name="rsq")
            alpha = keep.tile([P, L, 8], F32, name="alpha")
            lwls = keep.tile([P, L, NC], F32, name="lwls")
            lw_ps = psum.tile([P, P], BF16, name="lw_ps", tag="bank")
            r_row = [early.tile([P, G, 2, P, 2], F32, name="r_row%d" % l) for l in range(L)]
            for l in range(L):
                for g in range(G):
                    bank = psum.tile([P, 2, 2, P], F32, name="rb", tag="bank")
                    for j in range(4):
                        col = rcol[:, l, g, j : j + 1]
                        nc.tensor.transpose(bank[:, j % 2, j // 2, :], col.to_broadcast([P, P]), ident_f[:])
                    nc.scalar.copy(r_row[l][:, g], bank[:].rearrange("q e u p -> q u p e"))
            nc.tensor.transpose(lw_ps[:], lwrows[:], ident_b[:])
            nc.vector.tensor_tensor(
                whole[:],
                pos[:].unsqueeze(2).to_broadcast([P, 4, NHI]),
                freq[:, 0, 0:NHI].unsqueeze(1).to_broadcast([P, 4, NHI]),
                ALU.mult,
            )
            nc.vector.tensor_tensor(
                phase[:, 0],
                pos[:].unsqueeze(2).to_broadcast([P, 4, HALF]),
                freq[:, 1, :].unsqueeze(1).to_broadcast([P, 4, HALF]),
                ALU.mult,
            )
            nc.vector.tensor_copy(whole_i[:], whole[:])
            nc.vector.tensor_tensor(whole[:], whole[:], whole_i[:], ALU.subtract)
            nc.vector.tensor_tensor(rsq[:], rflat, ls[:].unsqueeze(2).to_broadcast([P, L, 8]), ALU.mult)
            nc.vector.tensor_tensor(phase[:, 0, :, 0:NHI], phase[:, 0, :, 0:NHI], whole[:], ALU.add)
            nc.vector.tensor_scalar(phase[:, 1], phase[:, 0], 0.25, None, ALU.add)
            nc.vector.tensor_tensor(rsq[:], rsq[:], rsq[:], ALU.mult)
            flat = "p a j i -> p (a j i)"
            nc.vector.scalar_tensor_tensor(
                nphase[:].rearrange(flat), phase[:].rearrange(flat), 0.5, phase[:].rearrange(flat), ALU.is_ge, ALU.subtract
            )
            for l in range(L):
                nc.vector.tensor_scalar(lwls[:, l, :], lw_ps[:, l * NC : (l + 1) * NC], ls[:, l : l + 1], None, ALU.mult)
            nc.vector.scalar_tensor_tensor(alpha[:], rsq[:], -1.0 / E, rflat, ALU.mult, ALU.mult)
            cos_t = early.tile([P, 4, HALF], F32, name="cos_t")
            sin_t = early.tile([P, 4, 2, HALF], F32, name="sin_t")
            nc.scalar.activation(cos_t[:], nphase[:, 1], ACT.Sin, scale=-2 * math.pi)
            nc.scalar.activation(sin_t[:, :, 0, :], nphase[:, 0], ACT.Sin, scale=2 * math.pi)
            nc.scalar.activation(sin_t[:, :, 1, :], nphase[:, 0], ACT.Sin, scale=-2 * math.pi)
            rope = [keep.tile([P, 4, 2, D], F32, name="rope%d" % l) for l in range(L)]
            for l in range(L):
                nc.gpsimd.tensor_tensor(
                    rope[l][:, :, 0, :].rearrange("p j (a i) -> p j a i", a=2),
                    cos_t[:].unsqueeze(2).to_broadcast([P, 4, 2, HALF]),
                    kw[:, l, :].rearrange("p (a i) -> p a i", a=2).unsqueeze(1).to_broadcast([P, 4, 2, HALF]),
                    ALU.mult,
                )
                for a in range(2):
                    nc.gpsimd.tensor_tensor(
                        rope[l][:, :, 1, HALF * a : HALF * (a + 1)],
                        sin_t[:, :, a, :],
                        kw[:, l, HALF * (1 - a) : HALF * (2 - a)].unsqueeze(1).to_broadcast([P, 4, HALF]),
                        ALU.mult,
                    )
            def normed_step(i):
                if i % 2 == 0 and i // 2 + 1 < NC:
                    x_turn(i // 2 + 1)
                if 2 <= i < 2 * NC + 2:
                    normed_turn(*divmod(i - 2, 2))

            def normed_vec(i):
                if i < 2 * NC:
                    normed_mul(*divmod(i, 2))

            def normed_q(i):
                if 4 <= i < 2 * NC + 4:
                    normed_quant(*divmod(i - 4, 2))

            x_turn(0)
            for j in range(4):
                square_sums(0, j)
            for i in range(6):
                normed_step(i)
                if i == 5:
                    stats(0, 0)
                normed_vec(i)
            w_group(0)
            normed_q(4)
            stats(0, 1)
            normed_q(5)
            for n in range(9):
                u, j = divmod(n, 4)
                items = (6 + 2 * n, 7 + 2 * n)
                rope_products(n)
                for i in items:
                    normed_step(i)
                if n in (1, 2):
                    dv_turn(0, n - 1)
                if n in (5, 6):
                    dv_turn(1, n - 5)
                if n in (3, 5, 7):
                    dk_turn((n - 3) // 4, ((n - 3) // 2) % 2)
                rope_sum(n)
                if n < 3:
                    square_sums(1, n)
                    if n == 2:
                        square_sums(1, 3)
                elif n < 7:
                    square_sums(2, n - 3)
                else:
                    square_sums(3, 2 * (n - 7))
                    square_sums(3, 2 * (n - 7) + 1)
                if j == 3:
                    stats(u + 1, 0)
                if n > 0:
                    key_grad(n - 1)
                if j == 3:
                    stats(u + 1, 1)
                if n < 7:
                    w_group(n + 1)
                if n in (2, 4):
                    load_w(n // 2 + 1)
                if n in (2, 6):
                    load_dv(n // 4 + 1)
                if n == 2:
                    load_k(2)
                if n == 4:
                    load_g(2)
                    load_k(3)
                if n == 8:
                    load_g(3)
                    dk_turn(1, 1)
                    dk_group(1)
                rope_add(n)
                for i in items:
                    normed_vec(i)
                if n < 8:
                    w_quant(n)
                normed_q(items[0])
                if n in (3, 7):
                    feature_quant(u, 1)
                normed_q(items[1])
                if n == 7:
                    token_quant(0)
                if n == 5:
                    dk_group(0)
                if n == 6:
                    feature_quant(0, 0)
        st["late"] = ctx.enter_context(tc.tile_pool(name="late", bufs=1))

        def turn_pair(g, j, hh):
            back_turn(g, j, hh, 1)
            back_turn(g, j, hh, 0)
            if g == 1 and TAILG:
                add_layers(j, hh, nc.gpsimd)

        def dot_pair(g, j, hh):
            dot(g, j, hh, 1)
            dot(g, j, hh, 0)
            if g == 1 and not TAILG:
                add_first_layer(g, j, hh)

        for n in range(9, 17):
            if n < 16:
                rope_products(n)
                rope_sum(n)
            if n in ON_GPSIMD:
                rope_add(n)
                if n > 11:
                    add_layers(n - 12, 0, nc.gpsimd)
            if n in (12, 13, 14, 15):
                hh, jp = divmod(n - 12, 2)
                dot_pair(0, 2 * jp, hh)
                dot_pair(0, 2 * jp + 1, hh)
            if n == 9:
                feature_quant(1, 0)
            if n in (9, 10):
                dv_turn(2, n - 9)
            if n == 10:
                load_dv(3)
            if n in (13, 14):
                dv_turn(3, n - 13)
            if n in (11, 13, 15):
                dk_turn(2 + (n - 11) // 4, ((n - 11) // 2) % 2)
            if n < 13:
                for c in (2 * (n - 9), 2 * (n - 9) + 1):
                    for l in range(L):
                        dnormed(0, c, l)
                        dnormed_out(c, l)
            if n in (11, 12, 13, 14):
                hh, jp = divmod(n - 11, 2)
                turn_pair(0, 2 * jp, hh)
                turn_pair(0, 2 * jp + 1, hh)
            if n == 15:
                for i in range(8):
                    weight_grad(0, i)
            if n == 16:
                for c in range(4):
                    dnormed(1, c, 0)
                    dnormed_out(c, 0)
            if n == 11:
                stats(3, 0)
            key_grad(n - 1)
            if n == 16:
                dk_turn(3, 1)
                dk_group(3)
            if n == 11:
                stats(3, 1)
            if n < 16 and n not in ON_GPSIMD:
                rope_add(n)
            if n == 13:
                dk_group(2)
            if n == 10:
                token_quant(1)
            if n in (11, 15):
                feature_quant((n - 3) // 4, 1)
            if n == 14:
                feature_quant(2, 0)
                token_quant(2)
            if n == 16:
                for jj in range(4):
                    dot_sum(jj)
        add_layers(0, nc.vector)
        add_layers(1, nc.vector)
        feature_quant(3, 0)
        finish(0, 0)
        for c in range(4):
            dnormed(1, c, 1)
            dnormed_out(c, 1)
        finish(0, 1)
        add_layers(2, nc.vector)
        add_layers(3, nc.vector)
        token_quant(3)
        finish(0, 2)
        for c in range(4, NC):
            turn_pair(1, c - 4, 0)
            for l in range(L):
                dnormed(1, c, l)
                dnormed_out(c, l)
            if c == 4:
                finish(0, 3)
            dot_pair(1, c - 4, 0)
        for jj in range(5):
            if jj < 4:
                turn_pair(1, jj, 1)
            if jj < 3:
                for i in range(3 * jj, min(3 * jj + 3, 8)):
                    weight_grad(1, i)
            if jj > 0:
                dot_sum(jj - 1)
            if jj < 4:
                dot_pair(1, jj, 1)
            if jj > 0:
                finish(1, jj - 1, 4 if jj == 4 else 1)
